import numpy as np
import ml_dtypes


def mxq(x, axis, fmt="e4m3"):
    dtype, down = {"e4m3": (ml_dtypes.float8_e4m3fn, 7), "e5m2": (ml_dtypes.float8_e5m2, 14)}[fmt]
    v = np.moveaxis(np.asarray(x, np.float32).astype(ml_dtypes.bfloat16).astype(np.float64), axis, -1)
    blocks = v.reshape(v.shape[:-1] + (-1, 32))
    amax = np.abs(blocks).max(-1, keepdims=True)
    byte = np.maximum(np.where(amax > 0, np.frexp(amax)[1] - 1 + 127, 0) - down, 1)
    scale = np.exp2(byte - 127.0)
    codes = (blocks / scale).astype(np.float32).astype(dtype).astype(np.float64)
    return np.moveaxis((codes * scale).reshape(v.shape), -1, axis)


WIDE = False


def mx_kscale(k):
    if not WIDE:
        return np.ones(k)
    levels = np.array([10, -10, 5, -5, 0])
    if k % 512:
        return np.exp2(np.random.permutation(np.resize(levels, k // 32))).repeat(32)
    a = np.empty((k // 512, 16))
    for p in range(k // 512):
        a[p, :8] = np.random.permutation(np.resize(levels, 8))
        for g in range(8):
            far = levels[np.abs(levels - a[p, g]) >= 10]
            a[p, g + 8] = far[np.random.randint(len(far))]
    return np.exp2(a.ravel()).repeat(32)


BF16 = ml_dtypes.bfloat16


def bf(x):
    return np.asarray(x, np.float32).astype(BF16)


def f64(x):
    return np.asarray(x).astype(np.float64)


M, B, I, H, O = 5, 2048, 128, 512, 64
O2 = 2 * O
EPS = 1e-6


def softplus(v):
    return np.maximum(v, 0.0) + np.log(1.0 + np.exp(-np.abs(v)))


def draw0():
    s, t = mx_kscale(H), mx_kscale(H)
    return {"h1": bf(np.maximum(np.random.standard_normal((M, B, H)), 0.0) * s),
            "W2": bf(np.random.standard_normal((M, H, H)) * 1.4 / np.sqrt(H) * t[None, :, None] / s[None, None, :]),
            "b2": bf(np.random.standard_normal((M, H)) * 0.3 * t),
            "W3": bf(np.random.standard_normal((M, O2, H)) * 1.4 / np.sqrt(H) / t[None, None, :]),
            "b3": bf(np.random.standard_normal((M, O2)) * 0.3)}


def core(h1, W2, b2, W3, b3):
    h2 = np.maximum((mxq(f64(h1), 2, "e4m3") @ mxq(f64(W2), 2, "e4m3").transpose(0, 2, 1)) + f64(b2)[:, None, :], 0.0)
    y = (mxq(h2, 2, "e4m3") @ mxq(f64(W3), 2, "e4m3").transpose(0, 2, 1)) + f64(b3)[:, None, :]
    means = y[:, :, :O]
    variances = softplus(y[:, :, O:]) + EPS
    mean = means.mean(axis=0)
    variance = (variances + means ** 2).mean(axis=0) - mean ** 2
    variance = np.maximum(variance, 0.0) + EPS
    return mean, variance


def e4m3fn_bytes(y):
    return np.clip(np.asarray(y, np.float64), -448.0, 448.0).astype(np.float32).astype(ml_dtypes.float8_e4m3fn).view(np.uint8)


def e4m3fn_values(b):
    return np.asarray(b, np.uint8).view(ml_dtypes.float8_e4m3fn).astype(np.float64)


def setup_inputs():
    d = draw0()
    x0 = np.asarray(d['h1']).astype(np.float64)
    s = (np.max(np.abs(x0), axis=(0, 1), keepdims=True) / 448.0).astype(np.float32)
    out = {}
    for k, v in d.items():
        if k == 'h1':
            out['h1_bytes'] = e4m3fn_bytes(x0 / s.astype(np.float64))
            out['h1_scale'] = s
        else:
            out[k] = v
    return out


def reference(h1_bytes, h1_scale, W2, b2, W3, b3):
    return core(e4m3fn_values(h1_bytes) * h1_scale.astype(np.float64), W2, b2, W3, b3)

@@ -1,0 +1,322 @@
+from contextlib import ExitStack
+
+import concourse.mybir as mybir
+from concourse.masks import make_identity
+
+M, B, H, O2 = 5, 2048, 512, 128
+O = 64
+P = 128
+CH = 512
+NCHUNK = B // CH
+F32 = mybir.dt.float32
+BF16 = mybir.dt.bfloat16
+U8 = mybir.dt.uint8
+U32 = mybir.dt.uint32
+FP8 = mybir.dt.float8_e4m3fn
+FP8X4 = mybir.dt.float8_e4m3fn_x4
+AF = mybir.ActivationFunctionType
+ALU = mybir.AluOpType
+FLOPS = 2 * M * B * H * (H + O2)
+
+CAST = ["S","S"]
+INTER = ["G","G","G","G"]
+
+
+def tile_gaussianmixturemlp_pa_kernel(tc, h1_bytes, h1_scale, W2, b2, W3, b3, out_0, out_1):
+    nc = tc.nc
+    units = [(c, m) for c in range(NCHUNK) for m in range(M)]
+    NU = len(units)
+    with ExitStack() as ctx:
+        const = ctx.enter_context(tc.tile_pool(name="const", bufs=1))
+        pool = ctx.enter_context(tc.tile_pool(name="pool", bufs=3))
+        psum = ctx.enter_context(tc.psum_pool(name="psum", bufs=1))
+        ctx.enter_context(tc.manual_schedule())
+
+        ident = const.tile([P, P], F32, name="ident")
+        make_identity(nc, ident[:])
+        sc = const.tile([P, 4], F32, name="sc")
+        b2s = const.tile([P, M, 4], BF16, name="b2s")
+        b3s = const.tile([P, M, O2], BF16, name="b3s")
+        bsum = const.tile([P, O2], F32, name="bsum")
+        w2c = [const.tile([P, H], U32, name=f"w2c{m}", align_bytes=64) for m in range(M)]
+        w2s = [const.tile([P, H], U8, name=f"w2s{m}", align_bytes=64) for m in range(M)]
+        w3c = [const.tile([P, O2], U32, name=f"w3c{m}", align_bytes=64) for m in range(M)]
+        w3s = [const.tile([P, O2], U8, name=f"w3s{m}", align_bytes=64) for m in range(M)]
+        prod = [const.tile([P, 4, O], F32, name=f"prod{c}") for c in range(NCHUNK)]
+        part = [const.tile([P, 4, O], F32, name=f"part{c}") for c in range(NCHUNK)]
+
+        live = {}
+
+        def load(u):
+            c, m = units[u]
+            t = pool.tile([P, 4 * H], U8, name="bytes_in", bufs=4, align_bytes=64)
+            src = h1_bytes[m, c * CH:(c + 1) * CH, :].rearrange("(p i) k -> p (i k)", i=4)
+            if u == 0:
+                for h in range(2):
+                    nc.sync.dma_start(out=t[:, h * 1024:(h + 1) * 1024], in_=src[:, h * 1024:(h + 1) * 1024])
+            else:
+                nc.sync.dma_start(out=t[:], in_=src)
+            live["b", u] = t
+
+        def wload(m):
+            t = pool.tile([P, 4 * H], BF16, name="w2raw", bufs=3, align_bytes=64)
+            src = W2[m].rearrange("(p t) k -> p (t k)", t=4)
+            for h in range(2):
+                nc.sync.dma_start(out=t[:, h * 1024:(h + 1) * 1024], in_=src[:, h * 1024:(h + 1) * 1024])
+            t3 = pool.tile([P, H], BF16, name="w3raw", bufs=3, align_bytes=64)
+            nc.sync.dma_start(out=t3[:], in_=W3[m])
+            live["w", m] = (t, t3)
+
+        def eng_copy(e, out, in_):
+            if e == "S":
+                nc.scalar.copy(out, in_)
+            elif e == "V":
+                nc.vector.tensor_copy(out=out, in_=in_)
+            else:
+                nc.gpsimd.tensor_copy(out=out, in_=in_)
+
+        def cast(u):
+            x = pool.tile([P, 4 * H], BF16, name="xb", bufs=3, align_bytes=64)
+            bt = live.pop(("b", u))
+            for h in range(2):
+                s = slice(h * 1024, (h + 1) * 1024)
+                eng_copy(CAST[h], x[:, s], bt[:, s].bitcast(FP8))
+            live["x", u] = x
+
+        def transposes(words, count, base, tag, bufs):
+            tr = psum.tile([P, 2, 256], F32, name=tag, bufs=bufs)
+            for w in range(2):
+                for i in range(count):
+                    o = (base + i) * 256
+                    nc.tensor.transpose(tr[:, w, i * 128:(i + 1) * 128], words[:, o + w:o + 256:2], ident[:])
+            return tr
+
+        def T(u):
+            words = live.pop(("x", u))[:].bitcast(F32)
+            live["tr", u] = [transposes(words, 2, 2 * h, "tr", 2) for h in range(2)]
+
+        def Prod(u, h):
+            if h == 0:
+                live["g1", u] = pool.tile([P, H, 4], BF16, name="g1", bufs=2, align_bytes=64)
+            g = live["g1", u]
+            tr = live["tr", u][h]
+            nc.vector.tensor_tensor(
+                out=g[:, h * 256:(h + 1) * 256, :].rearrange("p n (w e) -> p n w e", e=2),
+                in0=tr[:].bitcast(BF16).rearrange("p w (n e) -> p n w e", e=2),
+                in1=sc[:].rearrange("p (w e) -> p w e", e=2).unsqueeze(1).to_broadcast([P, 256, 2, 2]),
+                op=ALU.mult)
+
+        def Q1(u):
+            g = live.pop(("g1", u))
+            cd = pool.tile([P, CH], U32, name="h1c", bufs=2, align_bytes=64)
+            s = pool.tile([P, CH], U8, name="h1s", bufs=2, align_bytes=64)
+            nc.vector.quantize_mx(out=cd[:].bitcast(FP8X4), scales=s[:], in_=g[:].rearrange("p n t -> p (n t)"))
+            live["h1", u] = (cd, s)
+
+        def M1(u):
+            c, m = units[u]
+            cd, s = live.pop(("h1", u))
+            live["mm", u] = []
+            for t in range(4):
+                a = psum.tile([P, CH], F32, name="mm", bufs=4)
+                ts = slice(t * 128, (t + 1) * 128)
+                nc.tensor.matmul_mx(out=a[:], lhsT=w2c[m][:, ts].bitcast(FP8X4), lhsT_scale=w2s[m][:, ts],
+                                    rhs=cd[:].bitcast(FP8X4), rhs_scale=s[:], start=True, stop=True)
+                live["mm", u].append(a)
+
+        def R(u):
+            c, m = units[u]
+            pl = pool.tile([P, 4, CH], BF16, name="planes", bufs=2, align_bytes=64)
+            for t, a in enumerate(live.pop(("mm", u))):
+                nc.scalar.activation(out=pl[:, t, :], in_=a[:], func=AF.Relu, bias=b2s[:, m, t:t + 1])
+            live["pl", u] = pl
+
+        def I(u):
+            pl = live.pop(("pl", u))
+            g = pool.tile([P, CH, 4], BF16, name="g2", bufs=2, align_bytes=64)
+            runs = []
+            for q in range(4):
+                if runs and runs[-1][0] == INTER[q]:
+                    runs[-1][2] = q + 1
+                else:
+                    runs.append([INTER[q], q, q + 1])
+            for e, q0, q1 in runs:
+                s = slice(q0 * 128, q1 * 128)
+                o = g[:, s, :].rearrange("p (c i) t -> p c t i", i=4)
+                i_ = pl[:, :, s].rearrange("p t (c i) -> p c t i", i=4)
+                if e == "G":
+                  for q in range(q0, q1):
+                    s = slice(q * 128, (q + 1) * 128)
+                    o = g[:, s, :]
+                    i_ = pl[:, :, s].rearrange("p t n -> p n t")
+                    nc.gpsimd.tensor_scalar(out=o, in0=i_, scalar1=1.0, scalar2=0.0, op0=ALU.mult, op1=ALU.add)
+                else:
+                    eng_copy(e, o, i_)
+            live["g2", u] = g
+
+        def Q2(u):
+            g = live.pop(("g2", u))
+            cd = pool.tile([P, CH], U32, name="h2c", bufs=8, align_bytes=64)
+            s = pool.tile([P, CH], U8, name="h2s", bufs=8, align_bytes=64)
+            nc.vector.quantize_mx(out=cd[:].bitcast(FP8X4), scales=s[:], in_=g[:].rearrange("p n t -> p (n t)"))
+            live["h2", u] = (cd, s)
+
+        def mx2(out, u, i, start, stop):
+            c, m = units[u]
+            cd, s = live["h2", u]
+            ns = slice(i * 128, (i + 1) * 128)
+            nc.tensor.matmul_mx(out=out, lhsT=cd[:, ns].bitcast(FP8X4), lhsT_scale=s[:, ns],
+                                rhs=w3c[m][:].bitcast(FP8X4), rhs_scale=w3s[m][:], start=start, stop=stop)
+
+        def M2(u):
+            y = psum.tile([P, 4, O2], F32, name="y", bufs=1)
+            for i in range(4):
+                mx2(y[:, i, :], u, i, True, True)
+            live["y", u] = y
+
+        def E1(u):
+            c, m = units[u]
+            ys = pool.tile([P, 4, O2], F32, name="ys", bufs=2)
+            nc.vector.tensor_tensor(out=ys[:], in0=live.pop(("y", u))[:],
+                                    in1=b3s[:, m, :].unsqueeze(1).to_broadcast([P, 4, O2]), op=ALU.add)
+            live["ys", u] = ys
+
+        def NL(u):
+            ys = live.pop(("ys", u))
+            sa = pool.tile([P, 4, O2], F32, name="sa", bufs=2)
+            e = pool.tile([P, 4, O], F32, name="e", bufs=2)
+            nc.scalar.activation(out=sa[:, :, O:O2], in_=ys[:, :, O:O2], func=AF.Abs)
+            nc.scalar.activation(out=e[:], in_=sa[:, :, O:O2], func=AF.Exp, scale=-1.0)
+            nc.scalar.activation(out=sa[:, :, 0:O], in_=ys[:, :, 0:O], func=AF.Square)
+            live["sa", u] = sa
+            live["e", u] = e
+
+        def PR(u):
+            c, m = units[u]
+            e = live.pop(("e", u))
+            if m == 0:
+                nc.vector.tensor_scalar(out=prod[c][:], in0=e[:], scalar1=1.0, scalar2=None, op0=ALU.add)
+            else:
+                nc.vector.scalar_tensor_tensor(out=prod[c][:], in0=e[:], scalar=1.0, in1=prod[c][:],
+                                               op0=ALU.add, op1=ALU.mult)
+
+        def ACC(u):
+            c, m = units[u]
+            sa = live.pop(("sa", u))
+            if m == 0:
+                live["acc"] = psum.tile([P, 4 * O2], F32, name="acc", bufs=1)
+            nc.tensor.matmul(live["acc"][:], ident[:], sa[:].rearrange("p i o -> p (i o)"), start=(m == 0), stop=(m == M - 1))
+
+        def SUM(c):
+            s5 = psum.tile([P, 4, O2], F32, name="y", bufs=1)
+            for i in range(4):
+                for m in range(M):
+                    mx2(s5[:, i, :], c * M + m, i, m == 0, m == M - 1)
+            for m in range(M):
+                live.pop(("h2", c * M + m))
+            live["s5"] = s5
+
+        def FIN(c):
+            mb = pool.tile([P, 4, O2], F32, name="mb", bufs=2)
+            nc.vector.scalar_tensor_tensor(out=mb[:], in0=live.pop("s5")[:], scalar=1.0 / M,
+                                           in1=bsum[:].unsqueeze(1).to_broadcast([P, 4, O2]), op0=ALU.mult, op1=ALU.add)
+            nc.sync.dma_start(out=out_0[c * CH:(c + 1) * CH, :].rearrange("(p i) o -> p i o", i=4), in_=mb[:, :, 0:O])
+            msq = pool.tile([P, 4, O], F32, name="msq", bufs=2)
+            nc.scalar.activation(out=msq[:], in_=mb[:, :, 0:O], func=AF.Square)
+            acc = live.pop("acc")[:].rearrange("p (i o) -> p i o", i=4)
+            rr = pool.tile([P, 4, O], F32, name="rr", bufs=2)
+            nc.vector.scalar_tensor_tensor(out=rr[:], in0=acc[:, :, O:O2], scalar=1.0 / M, in1=mb[:, :, O:O2],
+                                           op0=ALU.mult, op1=ALU.add)
+            qq = pool.tile([P, 4, O], F32, name="qq", bufs=2)
+            nc.vector.scalar_tensor_tensor(out=qq[:], in0=acc[:, :, 0:O], scalar=1.0 / M, in1=msq[:],
+                                           op0=ALU.mult, op1=ALU.subtract)
+            nc.vector.scalar_tensor_tensor(out=part[c][:], in0=rr[:], scalar=0.5, in1=qq[:], op0=ALU.mult, op1=ALU.add)
+
+        def LAST(c):
+            L = pool.tile([P, 4, O], F32, name="L", bufs=2)
+            nc.scalar.activation(out=L[:], in_=prod[c][:], func=AF.Ln)
+            v = pool.tile([P, 4, O], F32, name="v", bufs=2)
+            nc.vector.scalar_tensor_tensor(out=v[:], in0=L[:], scalar=1.0 / M, in1=part[c][:], op0=ALU.mult, op1=ALU.add)
+            vo = pool.tile([P, 4, O], F32, name="vo", bufs=2)
+            nc.vector.tensor_scalar(out=vo[:], in0=v[:], scalar1=0.0, scalar2=1e-6, op0=ALU.max, op1=ALU.add)
+            nc.sync.dma_start(out=out_1[c * CH:(c + 1) * CH, :].rearrange("(p i) o -> p i o", i=4), in_=vo[:])
+
+        def WPREP(m):
+            t, t3 = live.pop(("w", m))
+            words = t[:].bitcast(F32)
+            g = pool.tile([P, H, 4], BF16, name="wg", bufs=2, align_bytes=64)
+            gw = g[:].rearrange("p n t -> p (n t)").bitcast(F32).rearrange("p (n w) -> p n w", w=2)
+            for h in range(2):
+                tr = transposes(words, 2, 2 * h, "mm", 4)
+                eng_copy("SV"[h], gw[:, h * 256:(h + 1) * 256, :], tr[:].rearrange("p w n -> p n w"))
+            g3 = pool.tile([P, O2, 4], BF16, name="wg3", bufs=2, align_bytes=64)
+            gw3 = g3[:].rearrange("p n t -> p (n t)").bitcast(F32).rearrange("p (n w) -> p n w", w=2)
+            tr = transposes(t3[:].bitcast(F32), 1, 0, "mm", 4)
+            eng_copy("S", gw3, tr[:, :, 0:O2].rearrange("p w n -> p n w"))
+            live["wg", m] = (g, g3)
+
+        def WQ(m):
+            g, g3 = live.pop(("wg", m))
+            nc.vector.quantize_mx(out=w2c[m][:].bitcast(FP8X4), scales=w2s[m][:], in_=g[:].rearrange("p n t -> p (n t)"))
+            nc.vector.quantize_mx(out=w3c[m][:].bitcast(FP8X4), scales=w3s[m][:], in_=g3[:].rearrange("p n t -> p (n t)"))
+
+        load(0)
+        wload(0)
+        nc.sync.dma_start(out=sc[:], in_=h1_scale.rearrange("a b (p t) -> p (a b t)", t=4))
+        nc.sync.dma_start(out=b2s[:], in_=b2.rearrange("m (p t) -> p m t", t=4))
+        load(1)
+        wload(1)
+        nc.sync.dma_start(out=b3s[:].rearrange("p m o -> p (m o)"), in_=b3.rearrange("m o -> (m o)").partition_broadcast(P))
+        load(2)
+        cast(0)
+        T(0)
+        WPREP(0)
+        cast(1)
+        ok = lambda u: 0 <= u < NU
+        for s in range(NU + 5):
+            if ok(s + 3):
+                load(s + 3)
+            if s + 2 < M:
+                wload(s + 2)
+            if ok(s - 1):
+                M1(s - 1)
+            if ok(s - 3):
+                M2(s - 3)
+            if ok(s - 4):
+                ACC(s - 4)
+            if ok(s):
+                Prod(s, 0)
+            if s == 0:
+                WQ(0)
+            if ok(s + 2):
+                cast(s + 2)
+            if ok(s - 2):
+                I(s - 2)
+            if ok(s - 3):
+                E1(s - 3)
+            if ok(s):
+                Prod(s, 1)
+            if ok(s - 3):
+                NL(s - 3)
+            if ok(s - 1):
+                R(s - 1)
+            if ok(s):
+                Q1(s)
+            if s == 1:
+                nc.vector.tensor_reduce(out=bsum[:], in_=b3s[:].rearrange("p m o -> p o m"), axis=mybir.AxisListType.X, op=ALU.add)
+                nc.vector.tensor_scalar(out=bsum[:, 0:O], in0=bsum[:, 0:O], scalar1=1.0 / M, scalar2=None, op0=ALU.mult)
+                nc.vector.tensor_scalar(out=bsum[:, O:O2], in0=bsum[:, O:O2], scalar1=1.0 / M, scalar2=2e-6, op0=ALU.mult, op1=ALU.add)
+            if ok(s - 4):
+                PR(s - 4)
+                if (s - 4) % M == M - 1:
+                    SUM((s - 4) // M)
+                    FIN((s - 4) // M)
+            if ok(s - 2):
+                Q2(s - 2)
+            if ok(s + 1):
+                T(s + 1)
+            if s + 1 < M:
+                WPREP(s + 1)
+                WQ(s + 1)
+        for c in range(NCHUNK - 1, -1, -1):
+            LAST(c)

@@ -18,8 +18,20 @@ AF = mybir.ActivationFunctionType
 ALU = mybir.AluOpType
 FLOPS = 2 * M * B * H * (H + O2)
 
-CAST = ["S","S"]
-INTER = ["G","G","G","G"]
+CAST = ["S","S","S","V"]
+INTER = ["G","G","G","G","G","G","G","G"]
+ORDER = [["load",3],["wload",2],["M1",-1],["M2",-3],["IV",-2],["P0",0],["GG",-3],["IG",-2],["E1",-3],["P1",0],["FINB",-5],["ACC",-4],["R",-1],["WT0",1],["WT1",1],["WT2",1],["WE0",1],["WE1",1],["WE2",1],["CS",2],["NL",-3],["CV",2],["FINC",-5],["Q1",0],["PR",-4],["WQ",1],["Q2",-2],["SUM",-4],["FINA",-4],["T0",1],["T1",1]]
+HEAD = [["load",0],["sc",0],["wload",0],["load",1],["b2",0],["wload",1],["b3",0],["load",2],["half",0],["CS",0],["CV",0],["T0",0],["T1",0],["WT0",0],["WT1",0],["WT2",0],["WE0",0],["WE1",0],["WE2",0],["CS",1],["CV",1],["bsum",0],["WQ",0]]
+CAST_U = {}
+INTER_U = {"18":["V","V","V","V","G","G","G","G"],"19":["V","V","V","V","V","S","S","S"]}
+R_U = {"19":"SVSV"}
+RSPEC = "SSSS"
+TRB = 2
+MMB = 4
+TAIL = [["M1",19],["M2",17],["IV",18],["IG",18],["E1",17],["R",19],["PR",16],["NL",17],["Q2",18],["ACC",16],["M2",18],["IV",19],["IS",19],["E1",18],["Q2",19],["NL",18],["PR",17],["ACC",17],["M2",19],["E1",19],["PR",18],["NL",19],["SUM",19],["LNTAB",0],["FINA",19],["ACC",18],["ACC",19],["PR",19],["FINB",19],["FINC",19],["LN",[3,4]],["LN",[0,3]],["LAST",[3,4]],["LAST",[0,3]]]
+GSPLIT = 8
+WE = "SSS"
+XROAD = "A2"
 
 
 def tile_gaussianmixturemlp_pa_kernel(tc, h1_bytes, h1_scale, W2, b2, W3, b3, out_0, out_1):
@@ -34,7 +46,8 @@ def tile_gaussianmixturemlp_pa_kernel(tc, h1_bytes, h1_scale, W2, b2, W3, b3, ou
 
         ident = const.tile([P, P], F32, name="ident")
         make_identity(nc, ident[:])
-        sc = const.tile([P, 4], F32, name="sc")
+        half = const.tile([P, P], F32, name="half")
+        sc = const.tile([P, 4, H], F32, name="sc") if XROAD == "A1" else const.tile([P, 4], F32, name="sc")
         b2s = const.tile([P, M, 4], BF16, name="b2s")
         b3s = const.tile([P, M, O2], BF16, name="b3s")
         bsum = const.tile([P, O2], F32, name="bsum")
@@ -42,8 +55,8 @@ def tile_gaussianmixturemlp_pa_kernel(tc, h1_bytes, h1_scale, W2, b2, W3, b3, ou
         w2s = [const.tile([P, H], U8, name=f"w2s{m}", align_bytes=64) for m in range(M)]
         w3c = [const.tile([P, O2], U32, name=f"w3c{m}", align_bytes=64) for m in range(M)]
         w3s = [const.tile([P, O2], U8, name=f"w3s{m}", align_bytes=64) for m in range(M)]
-        prod = [const.tile([P, 4, O], F32, name=f"prod{c}") for c in range(NCHUNK)]
-        part = [const.tile([P, 4, O], F32, name=f"part{c}") for c in range(NCHUNK)]
+        prod = const.tile([P, NCHUNK, 4, O], F32, name="prod")
+        part = const.tile([P, NCHUNK, 4, O], F32, name="part")
 
         live = {}
 
@@ -75,13 +88,40 @@ def tile_gaussianmixturemlp_pa_kernel(tc, h1_bytes, h1_scale, W2, b2, W3, b3, ou
             else:
                 nc.gpsimd.tensor_copy(out=out, in_=in_)
 
-        def cast(u):
-            x = pool.tile([P, 4 * H], BF16, name="xb", bufs=3, align_bytes=64)
-            bt = live.pop(("b", u))
-            for h in range(2):
-                s = slice(h * 1024, (h + 1) * 1024)
-                eng_copy(CAST[h], x[:, s], bt[:, s].bitcast(FP8))
-            live["x", u] = x
+        def runs_of(spec):
+            runs = []
+            for q, e in enumerate(spec):
+                if runs and runs[-1][0] == e:
+                    runs[-1][2] = q + 1
+                else:
+                    runs.append([e, q, q + 1])
+            return runs
+
+        def cast(u, who):
+            if ("x", u) not in live:
+                live["x", u] = pool.tile([P, 4 * H], BF16, name="xb", bufs=3, align_bytes=64)
+            x = live["x", u]
+            bt = live["b", u]
+            for e, q0, q1 in runs_of(CAST_U.get(str(u), CAST)):
+                if e == who:
+                    if u == 0:
+                        for q in range(q0, q1):
+                            s = slice(q * H, (q + 1) * H)
+                            eng_copy(e, x[:, s], bt[:, s].bitcast(FP8))
+                    else:
+                        s = slice(q0 * H, q1 * H)
+                        eng_copy(e, x[:, s], bt[:, s].bitcast(FP8))
+
+        def X(u, h):
+            if ("x", u) not in live:
+                live["x", u] = pool.tile([P, 4 * H], BF16, name="xb", bufs=2, align_bytes=64)
+            x = live["x", u]
+            bt = live["b", u]
+            n = 512 if u == 0 else 1024
+            for a in range(1024 * h, 1024 * (h + 1), n):
+                k0 = 0 if u == 0 else a // H
+                nc.vector.tensor_tensor(out=x[:, a:a + n], in0=bt[:, a:a + n].bitcast(FP8),
+                                        in1=sc[:, k0:k0 + n // H, :].rearrange("p i k -> p (i k)"), op=ALU.mult)
 
         def transposes(words, count, base, tag, bufs):
             tr = psum.tile([P, 2, 256], F32, name=tag, bufs=bufs)
@@ -91,20 +131,29 @@ def tile_gaussianmixturemlp_pa_kernel(tc, h1_bytes, h1_scale, W2, b2, W3, b3, ou
                     nc.tensor.transpose(tr[:, w, i * 128:(i + 1) * 128], words[:, o + w:o + 256:2], ident[:])
             return tr
 
-        def T(u):
-            words = live.pop(("x", u))[:].bitcast(F32)
-            live["tr", u] = [transposes(words, 2, 2 * h, "tr", 2) for h in range(2)]
+        def T(u, h):
+            words = live["x", u][:].bitcast(F32)
+            live["tr", u, h] = transposes(words, 2, 2 * h, "tr", TRB)
+
+        def words_of(g):
+            return g[:].rearrange("p n t -> p (n t)").bitcast(F32).rearrange("p (n w) -> p n w", w=2)
 
         def Prod(u, h):
             if h == 0:
-                live["g1", u] = pool.tile([P, H, 4], BF16, name="g1", bufs=2, align_bytes=64)
+                live["g1", u] = pool.tile([P, CH, 4], BF16, name="g1", bufs=2, align_bytes=64)
             g = live["g1", u]
-            tr = live["tr", u][h]
+            tr = live.pop(("tr", u, h))
             nc.vector.tensor_tensor(
                 out=g[:, h * 256:(h + 1) * 256, :].rearrange("p n (w e) -> p n w e", e=2),
                 in0=tr[:].bitcast(BF16).rearrange("p w (n e) -> p n w e", e=2),
                 in1=sc[:].rearrange("p (w e) -> p w e", e=2).unsqueeze(1).to_broadcast([P, 256, 2, 2]),
                 op=ALU.mult)
+
+        def EV(u, h):
+            if h == 0:
+                live["g1", u] = pool.tile([P, CH, 4], BF16, name="g1", bufs=2, align_bytes=64)
+            g = live["g1", u]
+            nc.scalar.copy(words_of(g)[:, h * 256:(h + 1) * 256, :], live.pop(("tr", u, h))[:].rearrange("p w n -> p n w"))
 
         def Q1(u):
             g = live.pop(("g1", u))
@@ -118,7 +167,7 @@ def tile_gaussianmixturemlp_pa_kernel(tc, h1_bytes, h1_scale, W2, b2, W3, b3, ou
             cd, s = live.pop(("h1", u))
             live["mm", u] = []
             for t in range(4):
-                a = psum.tile([P, CH], F32, name="mm", bufs=4)
+                a = psum.tile([P, CH], F32, name="mm", bufs=MMB)
                 ts = slice(t * 128, (t + 1) * 128)
                 nc.tensor.matmul_mx(out=a[:], lhsT=w2c[m][:, ts].bitcast(FP8X4), lhsT_scale=w2s[m][:, ts],
                                     rhs=cd[:].bitcast(FP8X4), rhs_scale=s[:], start=True, stop=True)
@@ -126,38 +175,37 @@ def tile_gaussianmixturemlp_pa_kernel(tc, h1_bytes, h1_scale, W2, b2, W3, b3, ou
 
         def R(u):
             c, m = units[u]
-            pl = pool.tile([P, 4, CH], BF16, name="planes", bufs=2, align_bytes=64)
+            pl = pool.tile([P, 4, CH], BF16, name="planes", bufs=3, align_bytes=64)
             for t, a in enumerate(live.pop(("mm", u))):
-                nc.scalar.activation(out=pl[:, t, :], in_=a[:], func=AF.Relu, bias=b2s[:, m, t:t + 1])
+                if R_U.get(str(u), RSPEC)[t] == "S":
+                    nc.scalar.activation(out=pl[:, t, :], in_=a[:], func=AF.Relu, bias=b2s[:, m, t:t + 1])
+                else:
+                    nc.vector.tensor_scalar(out=pl[:, t, :], in0=a[:], scalar1=b2s[:, m, t:t + 1], scalar2=0.0, op0=ALU.add, op1=ALU.max)
             live["pl", u] = pl
 
-        def I(u):
-            pl = live.pop(("pl", u))
-            g = pool.tile([P, CH, 4], BF16, name="g2", bufs=2, align_bytes=64)
-            runs = []
-            for q in range(4):
-                if runs and runs[-1][0] == INTER[q]:
-                    runs[-1][2] = q + 1
-                else:
-                    runs.append([INTER[q], q, q + 1])
-            for e, q0, q1 in runs:
-                s = slice(q0 * 128, q1 * 128)
-                o = g[:, s, :].rearrange("p (c i) t -> p c t i", i=4)
-                i_ = pl[:, :, s].rearrange("p t (c i) -> p c t i", i=4)
-                if e == "G":
-                  for q in range(q0, q1):
-                    s = slice(q * 128, (q + 1) * 128)
-                    o = g[:, s, :]
-                    i_ = pl[:, :, s].rearrange("p t n -> p n t")
-                    nc.gpsimd.tensor_scalar(out=o, in0=i_, scalar1=1.0, scalar2=0.0, op0=ALU.mult, op1=ALU.add)
-                else:
-                    eng_copy(e, o, i_)
-            live["g2", u] = g
+        def I(u, who):
+            pl = live["pl", u]
+            if ("g2", u) not in live:
+                live["g2", u] = pool.tile([P, CH, 4], BF16, name="g2", bufs=2, align_bytes=64)
+            g = live["g2", u]
+            for e, q0, q1 in runs_of(INTER_U.get(str(u), INTER)):
+                if e != who:
+                    continue
+                step = GSPLIT if e == "G" else q1 - q0
+                for q in range(q0, q1, step):
+                    s = slice(q * 64, min(q + step, q1) * 64)
+                    o = g[:, s, :].rearrange("p (c i) t -> p c t i", i=4)
+                    i_ = pl[:, :, s].rearrange("p t (c i) -> p c t i", i=4)
+                    if e == "G":
+                        nc.gpsimd.tensor_scalar(out=g[:, s, :], in0=pl[:, :, s].rearrange("p t n -> p n t"),
+                                                scalar1=1.0, scalar2=0.0, op0=ALU.mult, op1=ALU.add)
+                    else:
+                        eng_copy(e, o, i_)
 
         def Q2(u):
             g = live.pop(("g2", u))
-            cd = pool.tile([P, CH], U32, name="h2c", bufs=8, align_bytes=64)
-            s = pool.tile([P, CH], U8, name="h2s", bufs=8, align_bytes=64)
+            cd = pool.tile([P, CH], U32, name="h2c", bufs=10, align_bytes=64)
+            s = pool.tile([P, CH], U8, name="h2s", bufs=10, align_bytes=64)
             nc.vector.quantize_mx(out=cd[:].bitcast(FP8X4), scales=s[:], in_=g[:].rearrange("p n t -> p (n t)"))
             live["h2", u] = (cd, s)
 
@@ -176,36 +224,38 @@ def tile_gaussianmixturemlp_pa_kernel(tc, h1_bytes, h1_scale, W2, b2, W3, b3, ou
 
         def E1(u):
             c, m = units[u]
-            ys = pool.tile([P, 4, O2], F32, name="ys", bufs=2)
+            ys = pool.tile([P, 4, O2], F32, name="ys", bufs=3)
             nc.vector.tensor_tensor(out=ys[:], in0=live.pop(("y", u))[:],
                                     in1=b3s[:, m, :].unsqueeze(1).to_broadcast([P, 4, O2]), op=ALU.add)
             live["ys", u] = ys
 
         def NL(u):
             ys = live.pop(("ys", u))
-            sa = pool.tile([P, 4, O2], F32, name="sa", bufs=2)
-            e = pool.tile([P, 4, O], F32, name="e", bufs=2)
-            nc.scalar.activation(out=sa[:, :, O:O2], in_=ys[:, :, O:O2], func=AF.Abs)
-            nc.scalar.activation(out=e[:], in_=sa[:, :, O:O2], func=AF.Exp, scale=-1.0)
-            nc.scalar.activation(out=sa[:, :, 0:O], in_=ys[:, :, 0:O], func=AF.Square)
-            live["sa", u] = sa
+            sq = pool.tile([P, 4, O], F32, name="sq", bufs=3)
+            ab = pool.tile([P, 4, O], F32, name="ab", bufs=3)
+            e = pool.tile([P, 4, O], F32, name="e", bufs=3)
+            nc.scalar.activation(out=ab[:], in_=ys[:, :, O:O2], func=AF.Abs)
+            nc.scalar.activation(out=sq[:], in_=ys[:, :, 0:O], func=AF.Square)
+            nc.scalar.activation(out=e[:], in_=ab[:], func=AF.Exp, scale=-1.0)
+            live["sa", u] = (sq, ab)
             live["e", u] = e
 
         def PR(u):
             c, m = units[u]
             e = live.pop(("e", u))
             if m == 0:
-                nc.vector.tensor_scalar(out=prod[c][:], in0=e[:], scalar1=1.0, scalar2=None, op0=ALU.add)
+                nc.vector.tensor_scalar(out=prod[:, c, :, :], in0=e[:], scalar1=1.0, scalar2=None, op0=ALU.add)
             else:
-                nc.vector.scalar_tensor_tensor(out=prod[c][:], in0=e[:], scalar=1.0, in1=prod[c][:],
+                nc.vector.scalar_tensor_tensor(out=prod[:, c, :, :], in0=e[:], scalar=1.0, in1=prod[:, c, :, :],
                                                op0=ALU.add, op1=ALU.mult)
 
         def ACC(u):
             c, m = units[u]
-            sa = live.pop(("sa", u))
+            sq, ab = live.pop(("sa", u))
             if m == 0:
-                live["acc"] = psum.tile([P, 4 * O2], F32, name="acc", bufs=1)
-            nc.tensor.matmul(live["acc"][:], ident[:], sa[:].rearrange("p i o -> p (i o)"), start=(m == 0), stop=(m == M - 1))
+                live["acc"] = psum.tile([P, 4 * O], F32, name="acc", bufs=1)
+            nc.tensor.matmul(live["acc"][:], ident[:], sq[:].rearrange("p i o -> p (i o)"), start=(m == 0), stop=False)
+            nc.tensor.matmul(live["acc"][:], half[:], ab[:].rearrange("p i o -> p (i o)"), start=False, stop=(m == M - 1))
 
         def SUM(c):
             s5 = psum.tile([P, 4, O2], F32, name="y", bufs=1)
@@ -216,107 +266,130 @@ def tile_gaussianmixturemlp_pa_kernel(tc, h1_bytes, h1_scale, W2, b2, W3, b3, ou
                 live.pop(("h2", c * M + m))
             live["s5"] = s5
 
-        def FIN(c):
+        def FINA(c):
             mb = pool.tile([P, 4, O2], F32, name="mb", bufs=2)
             nc.vector.scalar_tensor_tensor(out=mb[:], in0=live.pop("s5")[:], scalar=1.0 / M,
                                            in1=bsum[:].unsqueeze(1).to_broadcast([P, 4, O2]), op0=ALU.mult, op1=ALU.add)
             nc.sync.dma_start(out=out_0[c * CH:(c + 1) * CH, :].rearrange("(p i) o -> p i o", i=4), in_=mb[:, :, 0:O])
             msq = pool.tile([P, 4, O], F32, name="msq", bufs=2)
             nc.scalar.activation(out=msq[:], in_=mb[:, :, 0:O], func=AF.Square)
+            live["fin"] = (mb, msq)
+
+        def FINB(c):
+            mb, msq = live["fin"]
             acc = live.pop("acc")[:].rearrange("p (i o) -> p i o", i=4)
-            rr = pool.tile([P, 4, O], F32, name="rr", bufs=2)
-            nc.vector.scalar_tensor_tensor(out=rr[:], in0=acc[:, :, O:O2], scalar=1.0 / M, in1=mb[:, :, O:O2],
-                                           op0=ALU.mult, op1=ALU.add)
             qq = pool.tile([P, 4, O], F32, name="qq", bufs=2)
-            nc.vector.scalar_tensor_tensor(out=qq[:], in0=acc[:, :, 0:O], scalar=1.0 / M, in1=msq[:],
-                                           op0=ALU.mult, op1=ALU.subtract)
-            nc.vector.scalar_tensor_tensor(out=part[c][:], in0=rr[:], scalar=0.5, in1=qq[:], op0=ALU.mult, op1=ALU.add)
+            nc.vector.scalar_tensor_tensor(out=qq[:], in0=acc, scalar=1.0 / M, in1=msq[:], op0=ALU.mult, op1=ALU.subtract)
+            live["qq"] = qq
 
-        def LAST(c):
-            L = pool.tile([P, 4, O], F32, name="L", bufs=2)
-            nc.scalar.activation(out=L[:], in_=prod[c][:], func=AF.Ln)
-            v = pool.tile([P, 4, O], F32, name="v", bufs=2)
-            nc.vector.scalar_tensor_tensor(out=v[:], in0=L[:], scalar=1.0 / M, in1=part[c][:], op0=ALU.mult, op1=ALU.add)
-            vo = pool.tile([P, 4, O], F32, name="vo", bufs=2)
-            nc.vector.tensor_scalar(out=vo[:], in0=v[:], scalar1=0.0, scalar2=1e-6, op0=ALU.max, op1=ALU.add)
-            nc.sync.dma_start(out=out_1[c * CH:(c + 1) * CH, :].rearrange("(p i) o -> p i o", i=4), in_=vo[:])
+        def FINC(c):
+            mb, msq = live.pop("fin")
+            qq = live.pop("qq")
+            nc.vector.scalar_tensor_tensor(out=part[:, c, :, :], in0=mb[:, :, O:O2], scalar=0.5, in1=qq[:], op0=ALU.mult, op1=ALU.add)
 
-        def WPREP(m):
-            t, t3 = live.pop(("w", m))
-            words = t[:].bitcast(F32)
-            g = pool.tile([P, H, 4], BF16, name="wg", bufs=2, align_bytes=64)
-            gw = g[:].rearrange("p n t -> p (n t)").bitcast(F32).rearrange("p (n w) -> p n w", w=2)
-            for h in range(2):
-                tr = transposes(words, 2, 2 * h, "mm", 4)
-                eng_copy("SV"[h], gw[:, h * 256:(h + 1) * 256, :], tr[:].rearrange("p w n -> p n w"))
-            g3 = pool.tile([P, O2, 4], BF16, name="wg3", bufs=2, align_bytes=64)
-            gw3 = g3[:].rearrange("p n t -> p (n t)").bitcast(F32).rearrange("p (n w) -> p n w", w=2)
-            tr = transposes(t3[:].bitcast(F32), 1, 0, "mm", 4)
-            eng_copy("S", gw3, tr[:, :, 0:O2].rearrange("p w n -> p n w"))
-            live["wg", m] = (g, g3)
+        def LN(c0, c1):
+            L = pool.tile([P, NCHUNK, 4, O], F32, name="L", bufs=1)
+            if "L" not in live:
+                live["L"] = L
+            L = live["L"]
+            nc.scalar.activation(out=L[:, c0:c1, :, :], in_=prod[:, c0:c1, :, :], func=AF.Ln)
+
+        def LNTAB():
+            d = pool.tile([P, 1], F32, name="lnd", bufs=1)
+            nc.scalar.activation(out=d[:], in_=prod[:, 0, 0, 0:1], func=AF.Ln)
+
+        def LAST(c0, c1):
+            L = live["L"]
+            v = pool.tile([P, 3, 4, O], F32, name="v", bufs=2)
+            n = c1 - c0
+            nc.vector.scalar_tensor_tensor(out=v[:, 0:n, :, :], in0=L[:, c0:c1, :, :], scalar=1.0 / M, in1=part[:, c0:c1, :, :], op0=ALU.mult, op1=ALU.add)
+            vo = pool.tile([P, 3, 4, O], F32, name="vo", bufs=2)
+            nc.vector.tensor_scalar(out=vo[:, 0:n, :, :], in0=v[:, 0:n, :, :], scalar1=0.0, scalar2=1e-6, op0=ALU.max, op1=ALU.add)
+            for c in range(c0, c1):
+                nc.sync.dma_start(out=out_1[c * CH:(c + 1) * CH, :].rearrange("(p i) o -> p i o", i=4), in_=vo[:, c - c0, :, :])
+
+        def WT(m, h):
+            t, t3 = live["w", m]
+            if h < 2:
+                live["wt", m, h] = transposes(t[:].bitcast(F32), 2, 2 * h, "mm", MMB)
+            else:
+                live["wt", m, h] = transposes(t3[:].bitcast(F32), 1, 0, "mm", MMB)
+
+        def WEV(m, h):
+            if ("wg", m) not in live:
+                live["wg", m] = (pool.tile([P, H, 4], BF16, name="wg", bufs=3, align_bytes=64),
+                                 pool.tile([P, O2, 4], BF16, name="wg3", bufs=3, align_bytes=64))
+            g, g3 = live["wg", m]
+            tr = live.pop(("wt", m, h))
+            if h < 2:
+                eng_copy(WE[h], words_of(g)[:, h * 256:(h + 1) * 256, :], tr[:].rearrange("p w n -> p n w"))
+            else:
+                eng_copy(WE[2], words_of(g3), tr[:, :, 0:O2].rearrange("p w n -> p n w"))
 
         def WQ(m):
             g, g3 = live.pop(("wg", m))
             nc.vector.quantize_mx(out=w2c[m][:].bitcast(FP8X4), scales=w2s[m][:], in_=g[:].rearrange("p n t -> p (n t)"))
             nc.vector.quantize_mx(out=w3c[m][:].bitcast(FP8X4), scales=w3s[m][:], in_=g3[:].rearrange("p n t -> p (n t)"))
 
-        load(0)
-        wload(0)
-        nc.sync.dma_start(out=sc[:], in_=h1_scale.rearrange("a b (p t) -> p (a b t)", t=4))
-        nc.sync.dma_start(out=b2s[:], in_=b2.rearrange("m (p t) -> p m t", t=4))
-        load(1)
-        wload(1)
-        nc.sync.dma_start(out=b3s[:].rearrange("p m o -> p (m o)"), in_=b3.rearrange("m o -> (m o)").partition_broadcast(P))
-        load(2)
-        cast(0)
-        T(0)
-        WPREP(0)
-        cast(1)
-        ok = lambda u: 0 <= u < NU
-        for s in range(NU + 5):
-            if ok(s + 3):
-                load(s + 3)
-            if s + 2 < M:
-                wload(s + 2)
-            if ok(s - 1):
-                M1(s - 1)
-            if ok(s - 3):
-                M2(s - 3)
-            if ok(s - 4):
-                ACC(s - 4)
-            if ok(s):
-                Prod(s, 0)
-            if s == 0:
-                WQ(0)
-            if ok(s + 2):
-                cast(s + 2)
-            if ok(s - 2):
-                I(s - 2)
-            if ok(s - 3):
-                E1(s - 3)
-            if ok(s):
-                Prod(s, 1)
-            if ok(s - 3):
-                NL(s - 3)
-            if ok(s - 1):
-                R(s - 1)
-            if ok(s):
-                Q1(s)
-            if s == 1:
-                nc.vector.tensor_reduce(out=bsum[:], in_=b3s[:].rearrange("p m o -> p o m"), axis=mybir.AxisListType.X, op=ALU.add)
-                nc.vector.tensor_scalar(out=bsum[:, 0:O], in0=bsum[:, 0:O], scalar1=1.0 / M, scalar2=None, op0=ALU.mult)
-                nc.vector.tensor_scalar(out=bsum[:, O:O2], in0=bsum[:, O:O2], scalar1=1.0 / M, scalar2=2e-6, op0=ALU.mult, op1=ALU.add)
-            if ok(s - 4):
-                PR(s - 4)
-                if (s - 4) % M == M - 1:
-                    SUM((s - 4) // M)
-                    FIN((s - 4) // M)
-            if ok(s - 2):
-                Q2(s - 2)
-            if ok(s + 1):
-                T(s + 1)
-            if s + 1 < M:
-                WPREP(s + 1)
-                WQ(s + 1)
-        for c in range(NCHUNK - 1, -1, -1):
-            LAST(c)
+        def scale_load():
+            if XROAD == "A1":
+                nc.sync.dma_start(out=sc[:, 0, :], in_=h1_scale.rearrange("a b k -> (a b k)").partition_broadcast(P))
+                for i in range(1, 4):
+                    nc.gpsimd.tensor_copy(out=sc[:, i, :], in_=sc[:, 0, :])
+            else:
+                nc.sync.dma_start(out=sc[:], in_=h1_scale.rearrange("a b (p t) -> p (a b t)", t=4))
+
+        def b2_load():
+            nc.sync.dma_start(out=b2s[:], in_=b2.rearrange("m (p t) -> p m t", t=4))
+
+        def b3_load():
+            nc.sync.dma_start(out=b3s[:].rearrange("p m o -> p (m o)"), in_=b3.rearrange("m o -> (m o)").partition_broadcast(P))
+
+        def bias_sum():
+            nc.vector.tensor_reduce(out=bsum[:], in_=b3s[:].rearrange("p m o -> p o m"), axis=mybir.AxisListType.X, op=ALU.add)
+            nc.vector.tensor_scalar(out=bsum[:, 0:O], in0=bsum[:, 0:O], scalar1=1.0 / M, scalar2=None, op0=ALU.mult)
+            nc.vector.tensor_scalar(out=bsum[:, O:O2], in0=bsum[:, O:O2], scalar1=1.0 / M, scalar2=2e-6, op0=ALU.mult, op1=ALU.add)
+
+        def GG(u):
+            gt = pool.tile([P, 1], U32, name="gt", bufs=2)
+            nc.gpsimd.tensor_copy(out=gt[:], in_=live["h2", u][0][:, 0:1])
+
+        def run(op, u):
+            if op in ("WQ", "wload"):
+                if 0 <= u < M:
+                    {"WQ": WQ, "wload": wload}[op](u)
+            elif op[:2] in ("WT", "WE"):
+                if 0 <= u < M:
+                    {"WT": WT, "WE": WEV}[op[:2]](u, int(op[2]))
+            elif op in ("SUM", "FINA", "FINB", "FINC"):
+                if 0 <= u < NU and u % M == M - 1:
+                    {"SUM": SUM, "FINA": FINA, "FINB": FINB, "FINC": FINC}[op](u // M)
+            elif op in ("sc", "b2", "b3"):
+                {"sc": scale_load, "b2": b2_load, "b3": b3_load}[op]()
+            elif op == "LAST":
+                LAST(*u)
+            elif op == "LN":
+                LN(*u)
+            elif op == "LNTAB":
+                LNTAB()
+            elif op == "half":
+                nc.gpsimd.tensor_scalar(out=half[:], in0=ident[:], scalar1=0.5, scalar2=0.0, op0=ALU.mult, op1=ALU.add)
+            elif op == "bsum":
+                if u == 0:
+                    bias_sum()
+            elif 0 <= u < NU:
+                f = {"load": load, "M1": M1, "M2": M2, "R": R, "Q1": Q1, "Q2": Q2, "E1": E1, "NL": NL, "PR": PR, "ACC": ACC, "GG": GG}
+                if op in f:
+                    f[op](u)
+                else:
+                    g = {"P": Prod, "X": X, "EV": EV, "T": T, "C": cast, "I": I}[op[0] if op[:2] != "EV" else "EV"]
+                    a = op[2:] if op[:2] == "EV" else op[1:]
+                    g(u, int(a) if a in ("0", "1") else a)
+
+        for op, u in HEAD:
+            run(op, u)
+        for s in range(NU):
+            for op, d in ORDER:
+                run(op, s + d)
+        for op, u in TAIL:
+            run(op, u)

@@ -20,15 +20,18 @@ FLOPS = 2 * M * B * H * (H + O2)
 
 CAST = ["S","S","S","V"]
 INTER = ["G","G","G","G","G","G","G","G"]
-ORDER = [["load",3],["wload",2],["M1",-1],["M2",-3],["IV",-2],["P0",0],["GG",-3],["IG",-2],["E1",-3],["P1",0],["FINB",-5],["ACC",-4],["R",-1],["WT0",1],["WT1",1],["WT2",1],["WE0",1],["WE1",1],["WE2",1],["CS",2],["NL",-3],["CV",2],["FINC",-5],["Q1",0],["PR",-4],["WQ",1],["Q2",-2],["SUM",-4],["FINA",-4],["T0",1],["T1",1]]
-HEAD = [["load",0],["sc",0],["wload",0],["load",1],["b2",0],["wload",1],["b3",0],["load",2],["half",0],["CS",0],["CV",0],["T0",0],["T1",0],["WT0",0],["WT1",0],["WT2",0],["WE0",0],["WE1",0],["WE2",0],["CS",1],["CV",1],["bsum",0],["WQ",0]]
-CAST_U = {}
+ORDER = [["M1",-1],["P0",0],["load",3],["M2",-3],["FINB",-5],["E1",-3],["GG",-3],["FINC",-5],["wload",2],["P1",0],["CV",2],["IG",-2],["R",-1],["WT0",1],["WT1",1],["ACC",-4],["WE1",1],["PR",-4],["Q1",0],["IS",-2],["IV",-2],["SUM",-4],["WT2",1],["WE0",1],["WE2",1],["NL",-3],["WQ",1],["T0",1],["Q2",-2],["T1",1],["CS",2],["FINA",-4]]
+HEAD = [["load",0],["wload",0],["b3",0],["sc",0],["CV",0],["load",1],["CS",0],["WT0",0],["T0",0],["WT1",0],["T1",0],["b2",0],["load",2],["wload",1],["WE0",0],["bsum",0],["CV",1],["WE1",0],["WT2",0],["WE2",0],["WQ",0],["CS",1]]
+CAST_U = {"0":["S","V","V","S"],"1":["S","S","V","V"],"4":["S","S","S","V"],"8":["S","S","S","V"],"13":["S","S","S","V"]}
 INTER_U = {"18":["V","V","V","V","G","G","G","G"],"19":["V","V","V","V","V","S","S","S"]}
 R_U = {"19":"SVSV"}
 RSPEC = "SSSS"
+PRG = []
+FCG = False
 TRB = 2
 MMB = 4
-TAIL = [["M1",19],["M2",17],["IV",18],["IG",18],["E1",17],["R",19],["PR",16],["NL",17],["Q2",18],["ACC",16],["M2",18],["IV",19],["IS",19],["E1",18],["Q2",19],["NL",18],["PR",17],["ACC",17],["M2",19],["E1",19],["PR",18],["NL",19],["SUM",19],["LNTAB",0],["FINA",19],["ACC",18],["ACC",19],["PR",19],["FINB",19],["FINC",19],["LN",[3,4]],["LN",[0,3]],["LAST",[3,4]],["LAST",[0,3]]]
+TAIL = [["M2",17],["IV",18],["PR",16],["M1",19],["E1",17],["IS",18],["R",19],["IG",18],["IG",19],["Q2",18],["ACC",16],["NL",17],["IS",19],["IV",19],["M2",18],["E1",18],["Q2",19],["ACC",17],["PR",17],["M2",19],["E1",19],["NL",18],["SUM",19],["PR",18],["NL",19],["ACC",18],["PR",19],["LN",[0,3]],["FINA",19],["LAST",[0,3]],["LNTAB",0],["ACC",19],["FINB",19],["LN",[3,4]],["FINC",19],["LAST",[3,4]]]
+WE_U = {"0":"VSV","1":"SSS"}
 GSPLIT = 8
 WE = "SSS"
 XROAD = "A2"
@@ -46,7 +49,6 @@ def tile_gaussianmixturemlp_pa_kernel(tc, h1_bytes, h1_scale, W2, b2, W3, b3, ou
 
         ident = const.tile([P, P], F32, name="ident")
         make_identity(nc, ident[:])
-        half = const.tile([P, P], F32, name="half")
         sc = const.tile([P, 4, H], F32, name="sc") if XROAD == "A1" else const.tile([P, 4], F32, name="sc")
         b2s = const.tile([P, M, 4], BF16, name="b2s")
         b3s = const.tile([P, M, O2], BF16, name="b3s")
@@ -59,6 +61,9 @@ def tile_gaussianmixturemlp_pa_kernel(tc, h1_bytes, h1_scale, W2, b2, W3, b3, ou
         part = const.tile([P, NCHUNK, 4, O], F32, name="part")
 
         live = {}
+        warm = const.tile([P, 1], F32, name="warm")
+        nc.vector.memset(warm[:], 0.0)
+        nc.scalar.activation(out=warm[:], in_=warm[:], func=AF.Sigmoid)
 
         def load(u):
             c, m = units[u]
@@ -229,33 +234,34 @@ def tile_gaussianmixturemlp_pa_kernel(tc, h1_bytes, h1_scale, W2, b2, W3, b3, ou
                                     in1=b3s[:, m, :].unsqueeze(1).to_broadcast([P, 4, O2]), op=ALU.add)
             live["ys", u] = ys
 
+        def e_tile():
+            et = pool.tile([P, 4, O], F32, name="et", bufs=3)
+            return et[:]
+
         def NL(u):
+            c, m = units[u]
             ys = live.pop(("ys", u))
-            sq = pool.tile([P, 4, O], F32, name="sq", bufs=3)
-            ab = pool.tile([P, 4, O], F32, name="ab", bufs=3)
-            e = pool.tile([P, 4, O], F32, name="e", bufs=3)
-            nc.scalar.activation(out=ab[:], in_=ys[:, :, O:O2], func=AF.Abs)
-            nc.scalar.activation(out=sq[:], in_=ys[:, :, 0:O], func=AF.Square)
-            nc.scalar.activation(out=e[:], in_=ab[:], func=AF.Exp, scale=-1.0)
-            live["sa", u] = (sq, ab)
+            sa = pool.tile([P, 2, 4, O], F32, name="sa", bufs=3)
+            e = prod[:, c, :, :] if m == 0 else e_tile()
+            nc.scalar.activation(out=sa[:, 1, :, :], in_=ys[:, :, O:O2], func=AF.Abs, scale=0.5)
+            nc.scalar.activation(out=sa[:, 0, :, :], in_=ys[:, :, 0:O], func=AF.Square)
+            nc.scalar.activation(out=e, in_=sa[:, 1, :, :], func=AF.Sigmoid, scale=2.0)
+            live["sa", u] = sa
             live["e", u] = e
 
         def PR(u):
             c, m = units[u]
             e = live.pop(("e", u))
-            if m == 0:
-                nc.vector.tensor_scalar(out=prod[:, c, :, :], in0=e[:], scalar1=1.0, scalar2=None, op0=ALU.add)
-            else:
-                nc.vector.scalar_tensor_tensor(out=prod[:, c, :, :], in0=e[:], scalar=1.0, in1=prod[:, c, :, :],
-                                               op0=ALU.add, op1=ALU.mult)
+            if m > 0:
+                eng = nc.gpsimd if m in PRG else nc.vector
+                eng.tensor_tensor(out=prod[:, c, :, :], in0=prod[:, c, :, :], in1=e, op=ALU.mult)
 
         def ACC(u):
             c, m = units[u]
-            sq, ab = live.pop(("sa", u))
+            sa = live.pop(("sa", u))
             if m == 0:
-                live["acc"] = psum.tile([P, 4 * O], F32, name="acc", bufs=1)
-            nc.tensor.matmul(live["acc"][:], ident[:], sq[:].rearrange("p i o -> p (i o)"), start=(m == 0), stop=False)
-            nc.tensor.matmul(live["acc"][:], half[:], ab[:].rearrange("p i o -> p (i o)"), start=False, stop=(m == M - 1))
+                live["acc"] = psum.tile([P, 8 * O], F32, name="acc", bufs=1)
+            nc.tensor.matmul(live["acc"][:], ident[:], sa[:].rearrange("p j i o -> p (j i o)"), start=(m == 0), stop=(m == M - 1))
 
         def SUM(c):
             s5 = psum.tile([P, 4, O2], F32, name="y", bufs=1)
@@ -268,8 +274,10 @@ def tile_gaussianmixturemlp_pa_kernel(tc, h1_bytes, h1_scale, W2, b2, W3, b3, ou
 
         def FINA(c):
             mb = pool.tile([P, 4, O2], F32, name="mb", bufs=2)
-            nc.vector.scalar_tensor_tensor(out=mb[:], in0=live.pop("s5")[:], scalar=1.0 / M,
-                                           in1=bsum[:].unsqueeze(1).to_broadcast([P, 4, O2]), op0=ALU.mult, op1=ALU.add)
+            s5 = live.pop("s5")
+            for a, f in ((0, 1.0 / M), (O, 0.5 / M)):
+                nc.vector.scalar_tensor_tensor(out=mb[:, :, a:a + O], in0=s5[:, :, a:a + O], scalar=f,
+                                               in1=bsum[:, a:a + O].unsqueeze(1).to_broadcast([P, 4, O]), op0=ALU.mult, op1=ALU.add)
             nc.sync.dma_start(out=out_0[c * CH:(c + 1) * CH, :].rearrange("(p i) o -> p i o", i=4), in_=mb[:, :, 0:O])
             msq = pool.tile([P, 4, O], F32, name="msq", bufs=2)
             nc.scalar.activation(out=msq[:], in_=mb[:, :, 0:O], func=AF.Square)
@@ -277,15 +285,18 @@ def tile_gaussianmixturemlp_pa_kernel(tc, h1_bytes, h1_scale, W2, b2, W3, b3, ou
 
         def FINB(c):
             mb, msq = live["fin"]
-            acc = live.pop("acc")[:].rearrange("p (i o) -> p i o", i=4)
+            acc = live.pop("acc")[:].rearrange("p (j i o) -> p j i o", j=2, i=4)
+            rr = pool.tile([P, 4, O], F32, name="rr", bufs=2)
+            nc.vector.scalar_tensor_tensor(out=rr[:], in0=acc[:, 1, :, :], scalar=1.0 / M, in1=msq[:], op0=ALU.mult, op1=ALU.subtract)
             qq = pool.tile([P, 4, O], F32, name="qq", bufs=2)
-            nc.vector.scalar_tensor_tensor(out=qq[:], in0=acc, scalar=1.0 / M, in1=msq[:], op0=ALU.mult, op1=ALU.subtract)
+            nc.vector.scalar_tensor_tensor(out=qq[:], in0=acc[:, 0, :, :], scalar=1.0 / M, in1=rr[:], op0=ALU.mult, op1=ALU.add)
             live["qq"] = qq
 
         def FINC(c):
             mb, msq = live.pop("fin")
             qq = live.pop("qq")
-            nc.vector.scalar_tensor_tensor(out=part[:, c, :, :], in0=mb[:, :, O:O2], scalar=0.5, in1=qq[:], op0=ALU.mult, op1=ALU.add)
+            eng = nc.gpsimd if FCG and c < NCHUNK - 1 else nc.vector
+            eng.tensor_tensor(out=part[:, c, :, :], in0=mb[:, :, O:O2], in1=qq[:], op=ALU.add)
 
         def LN(c0, c1):
             L = pool.tile([P, NCHUNK, 4, O], F32, name="L", bufs=1)
@@ -302,7 +313,7 @@ def tile_gaussianmixturemlp_pa_kernel(tc, h1_bytes, h1_scale, W2, b2, W3, b3, ou
             L = live["L"]
             v = pool.tile([P, 3, 4, O], F32, name="v", bufs=2)
             n = c1 - c0
-            nc.vector.scalar_tensor_tensor(out=v[:, 0:n, :, :], in0=L[:, c0:c1, :, :], scalar=1.0 / M, in1=part[:, c0:c1, :, :], op0=ALU.mult, op1=ALU.add)
+            nc.vector.scalar_tensor_tensor(out=v[:, 0:n, :, :], in0=L[:, c0:c1, :, :], scalar=-1.0 / M, in1=part[:, c0:c1, :, :], op0=ALU.mult, op1=ALU.add)
             vo = pool.tile([P, 3, 4, O], F32, name="vo", bufs=2)
             nc.vector.tensor_scalar(out=vo[:, 0:n, :, :], in0=v[:, 0:n, :, :], scalar1=0.0, scalar2=1e-6, op0=ALU.max, op1=ALU.add)
             for c in range(c0, c1):
@@ -322,9 +333,9 @@ def tile_gaussianmixturemlp_pa_kernel(tc, h1_bytes, h1_scale, W2, b2, W3, b3, ou
             g, g3 = live["wg", m]
             tr = live.pop(("wt", m, h))
             if h < 2:
-                eng_copy(WE[h], words_of(g)[:, h * 256:(h + 1) * 256, :], tr[:].rearrange("p w n -> p n w"))
+                eng_copy(WE_U.get(str(m), WE)[h], words_of(g)[:, h * 256:(h + 1) * 256, :], tr[:].rearrange("p w n -> p n w"))
             else:
-                eng_copy(WE[2], words_of(g3), tr[:, :, 0:O2].rearrange("p w n -> p n w"))
+                eng_copy(WE_U.get(str(m), WE)[2], words_of(g3), tr[:, :, 0:O2].rearrange("p w n -> p n w"))
 
         def WQ(m):
             g, g3 = live.pop(("wg", m))
@@ -348,7 +359,7 @@ def tile_gaussianmixturemlp_pa_kernel(tc, h1_bytes, h1_scale, W2, b2, W3, b3, ou
         def bias_sum():
             nc.vector.tensor_reduce(out=bsum[:], in_=b3s[:].rearrange("p m o -> p o m"), axis=mybir.AxisListType.X, op=ALU.add)
             nc.vector.tensor_scalar(out=bsum[:, 0:O], in0=bsum[:, 0:O], scalar1=1.0 / M, scalar2=None, op0=ALU.mult)
-            nc.vector.tensor_scalar(out=bsum[:, O:O2], in0=bsum[:, O:O2], scalar1=1.0 / M, scalar2=2e-6, op0=ALU.mult, op1=ALU.add)
+            nc.vector.tensor_scalar(out=bsum[:, O:O2], in0=bsum[:, O:O2], scalar1=0.5 / M, scalar2=1e-6, op0=ALU.mult, op1=ALU.add)
 
         def GG(u):
             gt = pool.tile([P, 1], U32, name="gt", bufs=2)
@@ -372,8 +383,6 @@ def tile_gaussianmixturemlp_pa_kernel(tc, h1_bytes, h1_scale, W2, b2, W3, b3, ou
                 LN(*u)
             elif op == "LNTAB":
                 LNTAB()
-            elif op == "half":
-                nc.gpsimd.tensor_scalar(out=half[:], in0=ident[:], scalar1=0.5, scalar2=0.0, op0=ALU.mult, op1=ALU.add)
             elif op == "bsum":
                 if u == 0:
                     bias_sum()

@@ -20,18 +20,18 @@ FLOPS = 2 * M * B * H * (H + O2)
 
 CAST = ["S","S","S","V"]
 INTER = ["G","G","G","G","G","G","G","G"]
-ORDER = [["M1",-1],["P0",0],["load",3],["M2",-3],["FINB",-5],["E1",-3],["GG",-3],["FINC",-5],["wload",2],["P1",0],["CV",2],["IG",-2],["R",-1],["WT0",1],["WT1",1],["ACC",-4],["WE1",1],["PR",-4],["Q1",0],["IS",-2],["IV",-2],["SUM",-4],["WT2",1],["WE0",1],["WE2",1],["NL",-3],["WQ",1],["T0",1],["Q2",-2],["T1",1],["CS",2],["FINA",-4]]
-HEAD = [["load",0],["wload",0],["b3",0],["sc",0],["CV",0],["load",1],["CS",0],["WT0",0],["T0",0],["WT1",0],["T1",0],["b2",0],["load",2],["wload",1],["WE0",0],["bsum",0],["CV",1],["WE1",0],["WT2",0],["WE2",0],["WQ",0],["CS",1]]
-CAST_U = {"0":["S","V","V","S"],"1":["S","S","V","V"],"4":["S","S","S","V"],"8":["S","S","S","V"],"13":["S","S","S","V"]}
-INTER_U = {"18":["V","V","V","V","G","G","G","G"],"19":["V","V","V","V","V","S","S","S"]}
+ORDER = [["M2",-3],["P0",0],["FINB",-5],["load",3],["M1",-1],["P1",0],["E1",-3],["R",-1],["SUM",-4],["WT0",1],["WE0",1],["WT1",1],["WE1",1],["WT2",1],["CV",2],["T0",1],["Q1",0],["WE2",1],["WQ",1],["CS",2],["IG",-2],["Q2",-2],["IS",-2],["ACC",-4],["wload",2],["PR",-4],["FINA",-4],["NL",-3],["IV",-2],["T1",1],["FINC",-5],["GG",-3]]
+HEAD = [["wload",0],["load",0],["load",1],["CS",0],["CV",0],["CS",1],["b2",0],["WT0",0],["WT2",0],["WE0",0],["WT1",0],["WE2",0],["WE1",0],["b3",0],["CV",1],["sc",0],["bsum",0],["T0",0],["load",2],["wload",1],["WQ",0],["T1",0]]
+CAST_U = {"0":["S","V","V","S"],"1":["S","S","V","V"],"2":["S","S","S","V"],"3":["S","S","S","V"],"4":["S","S","S","V"],"5":["S","S","S","V"],"6":["S","S","S","V"],"7":["S","S","S","V"],"8":["S","S","S","V"],"13":["S","S","S","V"],"14":["S","S","S","V"],"15":["S","S","S","V"],"16":["S","S","S","V"],"18":["S","S","S","V"],"19":["S","S","S","V"]}
+INTER_U = {"0":["G","G","G","G","G","G","G","G"],"1":["G","G","G","G","G","G","G","G"],"17":["G","G","G","G","G","G","G","G"],"18":["V","V","V","V","G","G","G","G"],"19":["V","V","V","V","V","S","S","S"]}
 R_U = {"19":"SVSV"}
 RSPEC = "SSSS"
 PRG = []
-FCG = False
+FCG = True
 TRB = 2
 MMB = 4
-TAIL = [["M2",17],["IV",18],["PR",16],["M1",19],["E1",17],["IS",18],["R",19],["IG",18],["IG",19],["Q2",18],["ACC",16],["NL",17],["IS",19],["IV",19],["M2",18],["E1",18],["Q2",19],["ACC",17],["PR",17],["M2",19],["E1",19],["NL",18],["SUM",19],["PR",18],["NL",19],["ACC",18],["PR",19],["LN",[0,3]],["FINA",19],["LAST",[0,3]],["LNTAB",0],["ACC",19],["FINB",19],["LN",[3,4]],["FINC",19],["LAST",[3,4]]]
-WE_U = {"0":"VSV","1":"SSS"}
+TAIL = [["M2",17],["E1",17],["NL",17],["IG",18],["M1",19],["R",19],["IS",18],["IS",19],["IV",18],["PR",16],["ACC",16],["Q2",18],["IV",19],["M2",18],["E1",18],["Q2",19],["ACC",17],["M2",19],["PR",17],["NL",18],["E1",19],["SUM",19],["ACC",18],["PR",18],["NL",19],["LN",[0,3]],["PR",19],["FINA",19],["LNTAB",0],["ACC",19],["LAST",[0,3]],["LN",[3,4]],["IG",19],["FINB",19],["FINC",19],["LAST",[3,4]]]
+WE_U = {"0":"VSV","1":"SSS","3":"SSS","4":"SSS"}
 GSPLIT = 8
 WE = "SSS"
 XROAD = "A2"
@@ -186,6 +186,31 @@ def tile_gaussianmixturemlp_pa_kernel(tc, h1_bytes, h1_scale, W2, b2, W3, b3, ou
                     nc.scalar.activation(out=pl[:, t, :], in_=a[:], func=AF.Relu, bias=b2s[:, m, t:t + 1])
                 else:
                     nc.vector.tensor_scalar(out=pl[:, t, :], in0=a[:], scalar1=b2s[:, m, t:t + 1], scalar2=0.0, op0=ALU.add, op1=ALU.max)
+            live["pl", u] = pl
+
+        def MR(u):
+            c, m = units[u]
+            cd, s = live.pop(("h1", u))
+            pl = pool.tile([P, 4, CH], BF16, name="planes", bufs=3, align_bytes=64)
+            banks = []
+
+            def evac(t):
+                a = banks[t]
+                if R_U.get(str(u), RSPEC)[t] == "S":
+                    nc.scalar.activation(out=pl[:, t, :], in_=a[:], func=AF.Relu, bias=b2s[:, m, t:t + 1])
+                else:
+                    nc.vector.tensor_scalar(out=pl[:, t, :], in0=a[:], scalar1=b2s[:, m, t:t + 1], scalar2=0.0, op0=ALU.add, op1=ALU.max)
+
+            for t in range(4):
+                a = psum.tile([P, CH], F32, name="mm", bufs=MMB)
+                ts = slice(t * 128, (t + 1) * 128)
+                nc.tensor.matmul_mx(out=a[:], lhsT=w2c[m][:, ts].bitcast(FP8X4), lhsT_scale=w2s[m][:, ts],
+                                    rhs=cd[:].bitcast(FP8X4), rhs_scale=s[:], start=True, stop=True)
+                banks.append(a)
+                if t == 2:
+                    evac(0)
+            for t in range(1, 4):
+                evac(t)
             live["pl", u] = pl
 
         def I(u, who):
@@ -387,7 +412,7 @@ def tile_gaussianmixturemlp_pa_kernel(tc, h1_bytes, h1_scale, W2, b2, W3, b3, ou
                 if u == 0:
                     bias_sum()
             elif 0 <= u < NU:
-                f = {"load": load, "M1": M1, "M2": M2, "R": R, "Q1": Q1, "Q2": Q2, "E1": E1, "NL": NL, "PR": PR, "ACC": ACC, "GG": GG}
+                f = {"load": load, "M1": M1, "M2": M2, "R": R, "Q1": Q1, "Q2": Q2, "E1": E1, "NL": NL, "PR": PR, "ACC": ACC, "GG": GG, "MR": MR}
                 if op in f:
                     f[op](u)
                 else:

@@ -3,11 +3,14 @@ from contextlib import ExitStack
 import concourse.mybir as mybir
 from concourse.masks import make_identity
 
-M, B, H, O2 = 5, 2048, 512, 128
-O = 64
+M, B, H, O = 5, 2048, 512, 64
+O2 = 2 * O
 P = 128
-CH = 512
-NCHUNK = B // CH
+SLOTS = 4
+CHUNK = SLOTS * P
+CHUNKS = B // CHUNK
+UNITS = CHUNKS * M
+EPS = 1e-6
 F32 = mybir.dt.float32
 BF16 = mybir.dt.bfloat16
 U8 = mybir.dt.uint8
@@ -18,29 +21,11 @@ AF = mybir.ActivationFunctionType
 ALU = mybir.AluOpType
 FLOPS = 2 * M * B * H * (H + O2)
 
-CAST = ["S","S","S","V"]
-INTER = ["G","G","G","G","G","G","G","G"]
-ORDER = [["M2",-3],["P0",0],["FINB",-5],["load",3],["M1",-1],["P1",0],["E1",-3],["R",-1],["SUM",-4],["WT0",1],["WE0",1],["WT1",1],["WE1",1],["WT2",1],["CV",2],["T0",1],["Q1",0],["WE2",1],["WQ",1],["CS",2],["IG",-2],["Q2",-2],["IS",-2],["ACC",-4],["wload",2],["PR",-4],["FINA",-4],["NL",-3],["IV",-2],["T1",1],["FINC",-5],["GG",-3]]
-HEAD = [["wload",0],["load",0],["load",1],["CS",0],["CV",0],["CS",1],["b2",0],["WT0",0],["WT2",0],["WE0",0],["WT1",0],["WE2",0],["WE1",0],["b3",0],["CV",1],["sc",0],["bsum",0],["T0",0],["load",2],["wload",1],["WQ",0],["T1",0]]
-CAST_U = {"0":["S","V","V","S"],"1":["S","S","V","V"],"2":["S","S","S","V"],"3":["S","S","S","V"],"4":["S","S","S","V"],"5":["S","S","S","V"],"6":["S","S","S","V"],"7":["S","S","S","V"],"8":["S","S","S","V"],"13":["S","S","S","V"],"14":["S","S","S","V"],"15":["S","S","S","V"],"16":["S","S","S","V"],"18":["S","S","S","V"],"19":["S","S","S","V"]}
-INTER_U = {"0":["G","G","G","G","G","G","G","G"],"1":["G","G","G","G","G","G","G","G"],"17":["G","G","G","G","G","G","G","G"],"18":["V","V","V","V","G","G","G","G"],"19":["V","V","V","V","V","S","S","S"]}
-R_U = {"19":"SVSV"}
-RSPEC = "SSSS"
-PRG = []
-FCG = True
-TRB = 2
-MMB = 4
-TAIL = [["M2",17],["E1",17],["NL",17],["IG",18],["M1",19],["R",19],["IS",18],["IS",19],["IV",18],["PR",16],["ACC",16],["Q2",18],["IV",19],["M2",18],["E1",18],["Q2",19],["ACC",17],["M2",19],["PR",17],["NL",18],["E1",19],["SUM",19],["ACC",18],["PR",18],["NL",19],["LN",[0,3]],["PR",19],["FINA",19],["LNTAB",0],["ACC",19],["LAST",[0,3]],["LN",[3,4]],["IG",19],["FINB",19],["FINC",19],["LAST",[3,4]]]
-WE_U = {"0":"VSV","1":"SSS","3":"SSS","4":"SSS"}
-GSPLIT = 8
-WE = "SSS"
-XROAD = "A2"
+WARM_UP_MATMULS = 4
 
 
 def tile_gaussianmixturemlp_pa_kernel(tc, h1_bytes, h1_scale, W2, b2, W3, b3, out_0, out_1):
     nc = tc.nc
-    units = [(c, m) for c in range(NCHUNK) for m in range(M)]
-    NU = len(units)
     with ExitStack() as ctx:
         const = ctx.enter_context(tc.tile_pool(name="const", bufs=1))
         pool = ctx.enter_context(tc.tile_pool(name="pool", bufs=3))
@@ -49,381 +34,377 @@ def tile_gaussianmixturemlp_pa_kernel(tc, h1_bytes, h1_scale, W2, b2, W3, b3, ou
 
         ident = const.tile([P, P], F32, name="ident")
         make_identity(nc, ident[:])
-        sc = const.tile([P, 4, H], F32, name="sc") if XROAD == "A1" else const.tile([P, 4], F32, name="sc")
-        b2s = const.tile([P, M, 4], BF16, name="b2s")
-        b3s = const.tile([P, M, O2], BF16, name="b3s")
-        bsum = const.tile([P, O2], F32, name="bsum")
-        w2c = [const.tile([P, H], U32, name=f"w2c{m}", align_bytes=64) for m in range(M)]
-        w2s = [const.tile([P, H], U8, name=f"w2s{m}", align_bytes=64) for m in range(M)]
-        w3c = [const.tile([P, O2], U32, name=f"w3c{m}", align_bytes=64) for m in range(M)]
-        w3s = [const.tile([P, O2], U8, name=f"w3s{m}", align_bytes=64) for m in range(M)]
-        prod = const.tile([P, NCHUNK, 4, O], F32, name="prod")
-        part = const.tile([P, NCHUNK, 4, O], F32, name="part")
+        scale = const.tile([P, 4], F32, name="scale")
+        b2_cols = const.tile([P, M, 4], BF16, name="b2_cols")
+        b3_rows = const.tile([P, M, O2], BF16, name="b3_rows")
+        b3_mean = const.tile([P, O2], F32, name="b3_mean")
+        w2_codes = [const.tile([P, H], U32, name=f"w2_codes{m}", align_bytes=64) for m in range(M)]
+        w2_scales = [const.tile([P, H], U8, name=f"w2_scales{m}", align_bytes=64) for m in range(M)]
+        w3_codes = [const.tile([P, O2], U32, name=f"w3_codes{m}", align_bytes=64) for m in range(M)]
+        w3_scales = [const.tile([P, O2], U8, name=f"w3_scales{m}", align_bytes=64) for m in range(M)]
+        sigmoids = const.tile([P, CHUNKS, SLOTS, O], F32, name="sigmoids")
+        partial = const.tile([P, CHUNKS, SLOTS, O], F32, name="partial")
+        logs = const.tile([P, CHUNKS, SLOTS, O], F32, name="logs")
 
-        live = {}
-        warm = const.tile([P, 1], F32, name="warm")
-        nc.vector.memset(warm[:], 0.0)
-        nc.scalar.activation(out=warm[:], in_=warm[:], func=AF.Sigmoid)
+        first = const.tile([P, 1], F32, name="first")
+        nc.vector.memset(first[:], 0.0)
+        nc.scalar.activation(out=first[:], in_=first[:], func=AF.Sigmoid)
 
-        def load(u):
-            c, m = units[u]
-            t = pool.tile([P, 4 * H], U8, name="bytes_in", bufs=4, align_bytes=64)
-            src = h1_bytes[m, c * CH:(c + 1) * CH, :].rearrange("(p i) k -> p (i k)", i=4)
-            if u == 0:
-                for h in range(2):
-                    nc.sync.dma_start(out=t[:, h * 1024:(h + 1) * 1024], in_=src[:, h * 1024:(h + 1) * 1024])
-            else:
-                nc.sync.dma_start(out=t[:], in_=src)
-            live["b", u] = t
+        raw_bytes, wide, turned, products, h1_mx, banks, planes, mixed, h2_mx = {}, {}, {}, {}, {}, {}, {}, {}, {}
+        y_banks, y_rows, squares, sigmoid_of, sums, ends, acc_of = {}, {}, {}, {}, {}, {}, {}
+        w_raw, w_turned, w_mixed = {}, {}, {}
 
-        def wload(m):
-            t = pool.tile([P, 4 * H], BF16, name="w2raw", bufs=3, align_bytes=64)
+
+        def load_bytes(u):
+            c, m = divmod(u, M)
+            bytes_in = pool.tile([P, SLOTS * H], U8, name="bytes_in", bufs=4, align_bytes=64)
+            src = h1_bytes[m, c * CHUNK:(c + 1) * CHUNK, :].rearrange("(p i) k -> p (i k)", i=SLOTS)
+            pieces = 2 if u == 0 else 1
+            width = SLOTS * H // pieces
+            for a in range(0, SLOTS * H, width):
+                nc.sync.dma_start(out=bytes_in[:, a:a + width], in_=src[:, a:a + width])
+            raw_bytes[u] = bytes_in
+
+        def load_weights(m):
+            w2 = pool.tile([P, 4 * H], BF16, name="w2", align_bytes=64)
             src = W2[m].rearrange("(p t) k -> p (t k)", t=4)
-            for h in range(2):
-                nc.sync.dma_start(out=t[:, h * 1024:(h + 1) * 1024], in_=src[:, h * 1024:(h + 1) * 1024])
-            t3 = pool.tile([P, H], BF16, name="w3raw", bufs=3, align_bytes=64)
-            nc.sync.dma_start(out=t3[:], in_=W3[m])
-            live["w", m] = (t, t3)
+            for a in range(0, 4 * H, 2 * H):
+                nc.sync.dma_start(out=w2[:, a:a + 2 * H], in_=src[:, a:a + 2 * H])
+            w3 = pool.tile([P, H], BF16, name="w3", align_bytes=64)
+            nc.sync.dma_start(out=w3[:], in_=W3[m])
+            w_raw[m] = (w2, w3)
 
-        def eng_copy(e, out, in_):
-            if e == "S":
-                nc.scalar.copy(out, in_)
-            elif e == "V":
-                nc.vector.tensor_copy(out=out, in_=in_)
-            else:
-                nc.gpsimd.tensor_copy(out=out, in_=in_)
+        def load_scale():
+            nc.sync.dma_start(out=scale[:], in_=h1_scale.rearrange("a b (p t) -> p (a b t)", t=4))
 
-        def runs_of(spec):
-            runs = []
-            for q, e in enumerate(spec):
-                if runs and runs[-1][0] == e:
-                    runs[-1][2] = q + 1
-                else:
-                    runs.append([e, q, q + 1])
-            return runs
+        def load_b2():
+            nc.sync.dma_start(out=b2_cols[:], in_=b2.rearrange("m (p t) -> p m t", t=4))
 
-        def cast(u, who):
-            if ("x", u) not in live:
-                live["x", u] = pool.tile([P, 4 * H], BF16, name="xb", bufs=3, align_bytes=64)
-            x = live["x", u]
-            bt = live["b", u]
-            for e, q0, q1 in runs_of(CAST_U.get(str(u), CAST)):
-                if e == who:
-                    if u == 0:
-                        for q in range(q0, q1):
-                            s = slice(q * H, (q + 1) * H)
-                            eng_copy(e, x[:, s], bt[:, s].bitcast(FP8))
-                    else:
-                        s = slice(q0 * H, q1 * H)
-                        eng_copy(e, x[:, s], bt[:, s].bitcast(FP8))
+        def load_b3():
+            nc.sync.dma_start(out=b3_rows[:].rearrange("p m o -> p (m o)"),
+                              in_=b3.rearrange("m o -> (m o)").partition_broadcast(P))
 
-        def X(u, h):
-            if ("x", u) not in live:
-                live["x", u] = pool.tile([P, 4 * H], BF16, name="xb", bufs=2, align_bytes=64)
-            x = live["x", u]
-            bt = live["b", u]
-            n = 512 if u == 0 else 1024
-            for a in range(1024 * h, 1024 * (h + 1), n):
-                k0 = 0 if u == 0 else a // H
-                nc.vector.tensor_tensor(out=x[:, a:a + n], in0=bt[:, a:a + n].bitcast(FP8),
-                                        in1=sc[:, k0:k0 + n // H, :].rearrange("p i k -> p (i k)"), op=ALU.mult)
+        def average_b3():
+            nc.vector.tensor_reduce(out=b3_mean[:], in_=b3_rows[:].rearrange("p m o -> p o m"),
+                                    axis=mybir.AxisListType.X, op=ALU.add)
+            nc.vector.tensor_scalar(out=b3_mean[:, 0:O], in0=b3_mean[:, 0:O], scalar1=1.0 / M, scalar2=None, op0=ALU.mult)
+            nc.vector.tensor_scalar(out=b3_mean[:, O:O2], in0=b3_mean[:, O:O2], scalar1=0.5 / M, scalar2=EPS,
+                                    op0=ALU.mult, op1=ALU.add)
 
-        def transposes(words, count, base, tag, bufs):
-            tr = psum.tile([P, 2, 256], F32, name=tag, bufs=bufs)
+
+        def turn(rows, groups, first_group, tag, bufs):
+            words = rows[:].bitcast(F32)
+            bank = psum.tile([P, 2, 2 * P], F32, name=tag, bufs=bufs)
             for w in range(2):
-                for i in range(count):
-                    o = (base + i) * 256
-                    nc.tensor.transpose(tr[:, w, i * 128:(i + 1) * 128], words[:, o + w:o + 256:2], ident[:])
-            return tr
+                for g in range(groups):
+                    start = (first_group + g) * (H // 2)
+                    nc.tensor.transpose(bank[:, w, g * P:(g + 1) * P], words[:, start + w:start + H // 2:2], ident[:])
+            return bank
 
-        def T(u, h):
-            words = live["x", u][:].bitcast(F32)
-            live["tr", u, h] = transposes(words, 2, 2 * h, "tr", TRB)
+        def word_pairs(tile):
+            return tile[:].rearrange("p n t -> p (n t)").bitcast(F32).rearrange("p (n w) -> p n w", w=2)
 
-        def words_of(g):
-            return g[:].rearrange("p n t -> p (n t)").bitcast(F32).rearrange("p (n w) -> p n w", w=2)
+        def turn_weights(m, part):
+            w2, w3 = w_raw[m]
+            if part < 2:
+                w_turned[m, part] = turn(w2, 2, 2 * part, "mm", 4)
+            else:
+                w_turned[m, part] = turn(w3, 1, 0, "mm", 4)
 
-        def Prod(u, h):
-            if h == 0:
-                live["g1", u] = pool.tile([P, CH, 4], BF16, name="g1", bufs=2, align_bytes=64)
-            g = live["g1", u]
-            tr = live.pop(("tr", u, h))
+        def copy_weights(m, part):
+            if m not in w_mixed:
+                w_mixed[m] = (pool.tile([P, H, 4], BF16, name="w2_mixed", align_bytes=64),
+                              pool.tile([P, O2, 4], BF16, name="w3_mixed", align_bytes=64))
+            w2_mixed, w3_mixed = w_mixed[m]
+            bank = w_turned.pop((m, part))
+            if part < 2:
+                nc.scalar.copy(word_pairs(w2_mixed)[:, part * 2 * P:(part + 1) * 2 * P, :], bank[:].rearrange("p w n -> p n w"))
+            else:
+                nc.scalar.copy(word_pairs(w3_mixed), bank[:, :, 0:O2].rearrange("p w n -> p n w"))
+
+        def quantize(codes, scales, mixed_tile):
+            nc.vector.quantize_mx(out=codes[:].bitcast(FP8X4), scales=scales[:], in_=mixed_tile[:].rearrange("p n t -> p (n t)"))
+
+        def quantize_weights(m):
+            w2_mixed, w3_mixed = w_mixed.pop(m)
+            quantize(w2_codes[m], w2_scales[m], w2_mixed)
+            quantize(w3_codes[m], w3_scales[m], w3_mixed)
+
+
+        def widen(u):
+            wide[u] = pool.tile([P, SLOTS * H], BF16, name="wide", align_bytes=64)
+            if u == 0:
+                for i in range(SLOTS):
+                    cols = slice(i * H, (i + 1) * H)
+                    if i in (0, 3):
+                        nc.scalar.copy(wide[u][:, cols], raw_bytes[u][:, cols].bitcast(FP8))
+                    else:
+                        nc.vector.tensor_copy(out=wide[u][:, cols], in_=raw_bytes[u][:, cols].bitcast(FP8))
+            else:
+                nc.scalar.copy(wide[u][:], raw_bytes[u][:].bitcast(FP8))
+
+        def turn_bytes(u, half):
+            turned[u, half] = turn(wide[u], 2, 2 * half, "turned", 2)
+
+        def multiply(u, half):
+            if half == 0:
+                products[u] = pool.tile([P, CHUNK, 4], BF16, name="products", bufs=2, align_bytes=64)
             nc.vector.tensor_tensor(
-                out=g[:, h * 256:(h + 1) * 256, :].rearrange("p n (w e) -> p n w e", e=2),
-                in0=tr[:].bitcast(BF16).rearrange("p w (n e) -> p n w e", e=2),
-                in1=sc[:].rearrange("p (w e) -> p w e", e=2).unsqueeze(1).to_broadcast([P, 256, 2, 2]),
+                out=products[u][:, half * 2 * P:(half + 1) * 2 * P, :].rearrange("p n (w e) -> p n w e", e=2),
+                in0=turned.pop((u, half))[:].bitcast(BF16).rearrange("p w (n e) -> p n w e", e=2),
+                in1=scale[:].rearrange("p (w e) -> p w e", e=2).unsqueeze(1).to_broadcast([P, 2 * P, 2, 2]),
                 op=ALU.mult)
 
-        def EV(u, h):
-            if h == 0:
-                live["g1", u] = pool.tile([P, CH, 4], BF16, name="g1", bufs=2, align_bytes=64)
-            g = live["g1", u]
-            nc.scalar.copy(words_of(g)[:, h * 256:(h + 1) * 256, :], live.pop(("tr", u, h))[:].rearrange("p w n -> p n w"))
+        def quantize_h1(u):
+            codes = pool.tile([P, CHUNK], U32, name="h1_codes", bufs=2, align_bytes=64)
+            scales = pool.tile([P, CHUNK], U8, name="h1_scales", bufs=2, align_bytes=64)
+            quantize(codes, scales, products.pop(u))
+            h1_mx[u] = (codes, scales)
 
-        def Q1(u):
-            g = live.pop(("g1", u))
-            cd = pool.tile([P, CH], U32, name="h1c", bufs=2, align_bytes=64)
-            s = pool.tile([P, CH], U8, name="h1s", bufs=2, align_bytes=64)
-            nc.vector.quantize_mx(out=cd[:].bitcast(FP8X4), scales=s[:], in_=g[:].rearrange("p n t -> p (n t)"))
-            live["h1", u] = (cd, s)
-
-        def M1(u):
-            c, m = units[u]
-            cd, s = live.pop(("h1", u))
-            live["mm", u] = []
+        def first_matmul(u):
+            m = u % M
+            codes, scales = h1_mx.pop(u)
+            banks[u] = []
             for t in range(4):
-                a = psum.tile([P, CH], F32, name="mm", bufs=MMB)
-                ts = slice(t * 128, (t + 1) * 128)
-                nc.tensor.matmul_mx(out=a[:], lhsT=w2c[m][:, ts].bitcast(FP8X4), lhsT_scale=w2s[m][:, ts],
-                                    rhs=cd[:].bitcast(FP8X4), rhs_scale=s[:], start=True, stop=True)
-                live["mm", u].append(a)
+                bank = psum.tile([P, CHUNK], F32, name="mm", bufs=4)
+                cols = slice(t * P, (t + 1) * P)
+                nc.tensor.matmul_mx(out=bank[:], lhsT=w2_codes[m][:, cols].bitcast(FP8X4), lhsT_scale=w2_scales[m][:, cols],
+                                    rhs=codes[:].bitcast(FP8X4), rhs_scale=scales[:], start=True, stop=True)
+                banks[u].append(bank)
 
-        def R(u):
-            c, m = units[u]
-            pl = pool.tile([P, 4, CH], BF16, name="planes", bufs=3, align_bytes=64)
-            for t, a in enumerate(live.pop(("mm", u))):
-                if R_U.get(str(u), RSPEC)[t] == "S":
-                    nc.scalar.activation(out=pl[:, t, :], in_=a[:], func=AF.Relu, bias=b2s[:, m, t:t + 1])
-                else:
-                    nc.vector.tensor_scalar(out=pl[:, t, :], in0=a[:], scalar1=b2s[:, m, t:t + 1], scalar2=0.0, op0=ALU.add, op1=ALU.max)
-            live["pl", u] = pl
+        def relu(u):
+            planes[u] = pool.tile([P, 4, CHUNK], BF16, name="planes", align_bytes=64)
+            for t, bank in enumerate(banks.pop(u)):
+                nc.scalar.activation(out=planes[u][:, t, :], in_=bank[:], func=AF.Relu, bias=b2_cols[:, u % M, t:t + 1])
 
-        def MR(u):
-            c, m = units[u]
-            cd, s = live.pop(("h1", u))
-            pl = pool.tile([P, 4, CH], BF16, name="planes", bufs=3, align_bytes=64)
-            banks = []
 
-            def evac(t):
-                a = banks[t]
-                if R_U.get(str(u), RSPEC)[t] == "S":
-                    nc.scalar.activation(out=pl[:, t, :], in_=a[:], func=AF.Relu, bias=b2s[:, m, t:t + 1])
-                else:
-                    nc.vector.tensor_scalar(out=pl[:, t, :], in0=a[:], scalar1=b2s[:, m, t:t + 1], scalar2=0.0, op0=ALU.add, op1=ALU.max)
+        def hold_gpsimd(u):
+            word = pool.tile([P, 1], U32, name="word", bufs=2)
+            nc.gpsimd.tensor_copy(out=word[:], in_=h2_mx[u][0][:, 0:1])
 
-            for t in range(4):
-                a = psum.tile([P, CH], F32, name="mm", bufs=MMB)
-                ts = slice(t * 128, (t + 1) * 128)
-                nc.tensor.matmul_mx(out=a[:], lhsT=w2c[m][:, ts].bitcast(FP8X4), lhsT_scale=w2s[m][:, ts],
-                                    rhs=cd[:].bitcast(FP8X4), rhs_scale=s[:], start=True, stop=True)
-                banks.append(a)
-                if t == 2:
-                    evac(0)
-            for t in range(1, 4):
-                evac(t)
-            live["pl", u] = pl
-
-        def I(u, who):
-            pl = live["pl", u]
-            if ("g2", u) not in live:
-                live["g2", u] = pool.tile([P, CH, 4], BF16, name="g2", bufs=2, align_bytes=64)
-            g = live["g2", u]
-            for e, q0, q1 in runs_of(INTER_U.get(str(u), INTER)):
-                if e != who:
-                    continue
-                step = GSPLIT if e == "G" else q1 - q0
-                for q in range(q0, q1, step):
-                    s = slice(q * 64, min(q + step, q1) * 64)
-                    o = g[:, s, :].rearrange("p (c i) t -> p c t i", i=4)
-                    i_ = pl[:, :, s].rearrange("p t (c i) -> p c t i", i=4)
-                    if e == "G":
-                        nc.gpsimd.tensor_scalar(out=g[:, s, :], in0=pl[:, :, s].rearrange("p t n -> p n t"),
-                                                scalar1=1.0, scalar2=0.0, op0=ALU.mult, op1=ALU.add)
+        def interleave(u):
+            mixed[u] = pool.tile([P, CHUNK, 4], BF16, name="mixed", bufs=2, align_bytes=64)
+            if u < UNITS - 2:
+                nc.gpsimd.tensor_scalar(out=mixed[u][:], in0=planes[u][:].rearrange("p t n -> p n t"),
+                                        scalar1=1.0, scalar2=0.0, op0=ALU.mult, op1=ALU.add)
+            else:
+                share = CHUNK if u == UNITS - 2 else CHUNK // 2
+                for a in range(0, CHUNK, share):
+                    dst = mixed[u][:, a:a + share, :].rearrange("p (c i) t -> p c t i", i=4)
+                    src = planes[u][:, :, a:a + share].rearrange("p t (c i) -> p c t i", i=4)
+                    if a == 0:
+                        nc.vector.tensor_copy(out=dst, in_=src)
                     else:
-                        eng_copy(e, o, i_)
+                        nc.scalar.copy(dst, src)
 
-        def Q2(u):
-            g = live.pop(("g2", u))
-            cd = pool.tile([P, CH], U32, name="h2c", bufs=10, align_bytes=64)
-            s = pool.tile([P, CH], U8, name="h2s", bufs=10, align_bytes=64)
-            nc.vector.quantize_mx(out=cd[:].bitcast(FP8X4), scales=s[:], in_=g[:].rearrange("p n t -> p (n t)"))
-            live["h2", u] = (cd, s)
+        def quantize_h2(u):
+            codes = pool.tile([P, CHUNK], U32, name="h2_codes", bufs=2 * M, align_bytes=64)
+            scales = pool.tile([P, CHUNK], U8, name="h2_scales", bufs=2 * M, align_bytes=64)
+            quantize(codes, scales, mixed.pop(u))
+            h2_mx[u] = (codes, scales)
 
-        def mx2(out, u, i, start, stop):
-            c, m = units[u]
-            cd, s = live["h2", u]
-            ns = slice(i * 128, (i + 1) * 128)
-            nc.tensor.matmul_mx(out=out, lhsT=cd[:, ns].bitcast(FP8X4), lhsT_scale=s[:, ns],
-                                rhs=w3c[m][:].bitcast(FP8X4), rhs_scale=w3s[m][:], start=start, stop=stop)
+        def second_pass(out, u, i, start, stop):
+            m = u % M
+            codes, scales = h2_mx[u]
+            cols = slice(i * P, (i + 1) * P)
+            nc.tensor.matmul_mx(out=out, lhsT=codes[:, cols].bitcast(FP8X4), lhsT_scale=scales[:, cols],
+                                rhs=w3_codes[m][:].bitcast(FP8X4), rhs_scale=w3_scales[m][:], start=start, stop=stop)
 
-        def M2(u):
-            y = psum.tile([P, 4, O2], F32, name="y", bufs=1)
-            for i in range(4):
-                mx2(y[:, i, :], u, i, True, True)
-            live["y", u] = y
+        def second_matmul(u):
+            y_banks[u] = psum.tile([P, SLOTS, O2], F32, name="y", bufs=1)
+            for i in range(SLOTS):
+                second_pass(y_banks[u][:, i, :], u, i, True, True)
 
-        def E1(u):
-            c, m = units[u]
-            ys = pool.tile([P, 4, O2], F32, name="ys", bufs=3)
-            nc.vector.tensor_tensor(out=ys[:], in0=live.pop(("y", u))[:],
-                                    in1=b3s[:, m, :].unsqueeze(1).to_broadcast([P, 4, O2]), op=ALU.add)
-            live["ys", u] = ys
-
-        def e_tile():
-            et = pool.tile([P, 4, O], F32, name="et", bufs=3)
-            return et[:]
-
-        def NL(u):
-            c, m = units[u]
-            ys = live.pop(("ys", u))
-            sa = pool.tile([P, 2, 4, O], F32, name="sa", bufs=3)
-            e = prod[:, c, :, :] if m == 0 else e_tile()
-            nc.scalar.activation(out=sa[:, 1, :, :], in_=ys[:, :, O:O2], func=AF.Abs, scale=0.5)
-            nc.scalar.activation(out=sa[:, 0, :, :], in_=ys[:, :, 0:O], func=AF.Square)
-            nc.scalar.activation(out=e, in_=sa[:, 1, :, :], func=AF.Sigmoid, scale=2.0)
-            live["sa", u] = sa
-            live["e", u] = e
-
-        def PR(u):
-            c, m = units[u]
-            e = live.pop(("e", u))
-            if m > 0:
-                eng = nc.gpsimd if m in PRG else nc.vector
-                eng.tensor_tensor(out=prod[:, c, :, :], in0=prod[:, c, :, :], in1=e, op=ALU.mult)
-
-        def ACC(u):
-            c, m = units[u]
-            sa = live.pop(("sa", u))
-            if m == 0:
-                live["acc"] = psum.tile([P, 8 * O], F32, name="acc", bufs=1)
-            nc.tensor.matmul(live["acc"][:], ident[:], sa[:].rearrange("p j i o -> p (j i o)"), start=(m == 0), stop=(m == M - 1))
-
-        def SUM(c):
-            s5 = psum.tile([P, 4, O2], F32, name="y", bufs=1)
-            for i in range(4):
+        def sum_models(c):
+            sums[c] = psum.tile([P, SLOTS, O2], F32, name="y", bufs=1)
+            for i in range(SLOTS):
                 for m in range(M):
-                    mx2(s5[:, i, :], c * M + m, i, m == 0, m == M - 1)
-            for m in range(M):
-                live.pop(("h2", c * M + m))
-            live["s5"] = s5
+                    second_pass(sums[c][:, i, :], c * M + m, i, m == 0, m == M - 1)
 
-        def FINA(c):
-            mb = pool.tile([P, 4, O2], F32, name="mb", bufs=2)
-            s5 = live.pop("s5")
-            for a, f in ((0, 1.0 / M), (O, 0.5 / M)):
-                nc.vector.scalar_tensor_tensor(out=mb[:, :, a:a + O], in0=s5[:, :, a:a + O], scalar=f,
-                                               in1=bsum[:, a:a + O].unsqueeze(1).to_broadcast([P, 4, O]), op0=ALU.mult, op1=ALU.add)
-            nc.sync.dma_start(out=out_0[c * CH:(c + 1) * CH, :].rearrange("(p i) o -> p i o", i=4), in_=mb[:, :, 0:O])
-            msq = pool.tile([P, 4, O], F32, name="msq", bufs=2)
-            nc.scalar.activation(out=msq[:], in_=mb[:, :, 0:O], func=AF.Square)
-            live["fin"] = (mb, msq)
 
-        def FINB(c):
-            mb, msq = live["fin"]
-            acc = live.pop("acc")[:].rearrange("p (j i o) -> p j i o", j=2, i=4)
-            rr = pool.tile([P, 4, O], F32, name="rr", bufs=2)
-            nc.vector.scalar_tensor_tensor(out=rr[:], in0=acc[:, 1, :, :], scalar=1.0 / M, in1=msq[:], op0=ALU.mult, op1=ALU.subtract)
-            qq = pool.tile([P, 4, O], F32, name="qq", bufs=2)
-            nc.vector.scalar_tensor_tensor(out=qq[:], in0=acc[:, 0, :, :], scalar=1.0 / M, in1=rr[:], op0=ALU.mult, op1=ALU.add)
-            live["qq"] = qq
+        def add_b3(u):
+            y_rows[u] = pool.tile([P, SLOTS, O2], F32, name="y_rows")
+            nc.vector.tensor_tensor(out=y_rows[u][:], in0=y_banks.pop(u)[:],
+                                    in1=b3_rows[:, u % M, :].unsqueeze(1).to_broadcast([P, SLOTS, O2]), op=ALU.add)
 
-        def FINC(c):
-            mb, msq = live.pop("fin")
-            qq = live.pop("qq")
-            eng = nc.gpsimd if FCG and c < NCHUNK - 1 else nc.vector
-            eng.tensor_tensor(out=part[:, c, :, :], in0=mb[:, :, O:O2], in1=qq[:], op=ALU.add)
+        def nonlinear(u):
+            c, m = divmod(u, M)
+            y = y_rows.pop(u)
+            squares[u] = pool.tile([P, 2, SLOTS, O], F32, name="squares")
+            if m == 0:
+                sigmoid_of[u] = sigmoids[:, c, :, :]
+            else:
+                sigmoid_tile = pool.tile([P, SLOTS, O], F32, name="sigmoid_tile")
+                sigmoid_of[u] = sigmoid_tile[:]
+            nc.scalar.activation(out=squares[u][:, 1, :, :], in_=y[:, :, O:O2], func=AF.Abs, scale=0.5)
+            nc.scalar.activation(out=squares[u][:, 0, :, :], in_=y[:, :, 0:O], func=AF.Square)
+            nc.scalar.activation(out=sigmoid_of[u], in_=squares[u][:, 1, :, :], func=AF.Sigmoid, scale=2.0)
 
-        def LN(c0, c1):
-            L = pool.tile([P, NCHUNK, 4, O], F32, name="L", bufs=1)
-            if "L" not in live:
-                live["L"] = L
-            L = live["L"]
-            nc.scalar.activation(out=L[:, c0:c1, :, :], in_=prod[:, c0:c1, :, :], func=AF.Ln)
+        def multiply_sigmoids(u):
+            c, m = divmod(u, M)
+            factor = sigmoid_of.pop(u)
+            if m > 0:
+                nc.vector.tensor_tensor(out=sigmoids[:, c, :, :], in0=sigmoids[:, c, :, :], in1=factor, op=ALU.mult)
 
-        def LNTAB():
-            d = pool.tile([P, 1], F32, name="lnd", bufs=1)
-            nc.scalar.activation(out=d[:], in_=prod[:, 0, 0, 0:1], func=AF.Ln)
+        def add_squares(u):
+            c, m = divmod(u, M)
+            if m == 0:
+                acc_of[c] = psum.tile([P, 2 * SLOTS * O], F32, name="acc", bufs=1)
+            nc.tensor.matmul(acc_of[c][:], ident[:], squares.pop(u)[:].rearrange("p j i o -> p (j i o)"),
+                             start=(m == 0), stop=(m == M - 1))
 
-        def LAST(c0, c1):
-            L = live["L"]
-            v = pool.tile([P, 3, 4, O], F32, name="v", bufs=2)
+        def finish_mean(c):
+            averages = pool.tile([P, SLOTS, O2], F32, name="averages", bufs=2)
+            total = sums.pop(c)
+            for a, factor in ((0, 1.0 / M), (O, 0.5 / M)):
+                nc.vector.scalar_tensor_tensor(out=averages[:, :, a:a + O], in0=total[:, :, a:a + O], scalar=factor,
+                                               in1=b3_mean[:, a:a + O].unsqueeze(1).to_broadcast([P, SLOTS, O]),
+                                               op0=ALU.mult, op1=ALU.add)
+            nc.sync.dma_start(out=out_0[c * CHUNK:(c + 1) * CHUNK, :].rearrange("(p i) o -> p i o", i=SLOTS),
+                              in_=averages[:, :, 0:O])
+            mean_squared = pool.tile([P, SLOTS, O], F32, name="mean_squared", bufs=2)
+            nc.scalar.activation(out=mean_squared[:], in_=averages[:, :, 0:O], func=AF.Square)
+            ends[c] = (averages, mean_squared)
+
+        def finish_squares(c):
+            averages, mean_squared = ends[c]
+            acc = acc_of.pop(c)[:].rearrange("p (j i o) -> p j i o", j=2, i=SLOTS)
+            less = pool.tile([P, SLOTS, O], F32, name="less", bufs=2)
+            nc.vector.scalar_tensor_tensor(out=less[:], in0=acc[:, 1, :, :], scalar=1.0 / M, in1=mean_squared[:],
+                                           op0=ALU.mult, op1=ALU.subtract)
+            more = pool.tile([P, SLOTS, O], F32, name="more", bufs=2)
+            nc.vector.scalar_tensor_tensor(out=more[:], in0=acc[:, 0, :, :], scalar=1.0 / M, in1=less[:],
+                                           op0=ALU.mult, op1=ALU.add)
+            ends[c] = (averages, more)
+
+        def finish_partial(c):
+            averages, more = ends.pop(c)
+            engine = nc.gpsimd if c < CHUNKS - 1 else nc.vector
+            engine.tensor_tensor(out=partial[:, c, :, :], in0=averages[:, :, O:O2], in1=more[:], op=ALU.add)
+
+        def logarithm(c0, c1):
+            nc.scalar.activation(out=logs[:, c0:c1, :, :], in_=sigmoids[:, c0:c1, :, :], func=AF.Ln)
+
+        def finish_variance(c0, c1):
+            variance = pool.tile([P, CHUNKS - 1, SLOTS, O], F32, name="variance", bufs=2)
+            clipped = pool.tile([P, CHUNKS - 1, SLOTS, O], F32, name="clipped", bufs=2)
             n = c1 - c0
-            nc.vector.scalar_tensor_tensor(out=v[:, 0:n, :, :], in0=L[:, c0:c1, :, :], scalar=-1.0 / M, in1=part[:, c0:c1, :, :], op0=ALU.mult, op1=ALU.add)
-            vo = pool.tile([P, 3, 4, O], F32, name="vo", bufs=2)
-            nc.vector.tensor_scalar(out=vo[:, 0:n, :, :], in0=v[:, 0:n, :, :], scalar1=0.0, scalar2=1e-6, op0=ALU.max, op1=ALU.add)
+            nc.vector.scalar_tensor_tensor(out=variance[:, 0:n, :, :], in0=logs[:, c0:c1, :, :], scalar=-1.0 / M,
+                                           in1=partial[:, c0:c1, :, :], op0=ALU.mult, op1=ALU.add)
+            nc.vector.tensor_scalar(out=clipped[:, 0:n, :, :], in0=variance[:, 0:n, :, :], scalar1=0.0, scalar2=EPS,
+                                    op0=ALU.max, op1=ALU.add)
             for c in range(c0, c1):
-                nc.sync.dma_start(out=out_1[c * CH:(c + 1) * CH, :].rearrange("(p i) o -> p i o", i=4), in_=vo[:, c - c0, :, :])
+                nc.sync.dma_start(out=out_1[c * CHUNK:(c + 1) * CHUNK, :].rearrange("(p i) o -> p i o", i=SLOTS),
+                                  in_=clipped[:, c - c0, :, :])
 
-        def WT(m, h):
-            t, t3 = live["w", m]
-            if h < 2:
-                live["wt", m, h] = transposes(t[:].bitcast(F32), 2, 2 * h, "mm", MMB)
-            else:
-                live["wt", m, h] = transposes(t3[:].bitcast(F32), 1, 0, "mm", MMB)
+        def warm_up():
+            zeros = const.tile([P, CHUNK], BF16, name="zeros")
+            nc.vector.memset(zeros[:], 0.0)
+            bank = psum.tile([P, CHUNK], F32, name="y", bufs=1)
+            for i in range(WARM_UP_MATMULS):
+                nc.tensor.matmul(bank[:], zeros[:, 0:P], zeros[:], start=True, stop=True)
 
-        def WEV(m, h):
-            if ("wg", m) not in live:
-                live["wg", m] = (pool.tile([P, H, 4], BF16, name="wg", bufs=3, align_bytes=64),
-                                 pool.tile([P, O2, 4], BF16, name="wg3", bufs=3, align_bytes=64))
-            g, g3 = live["wg", m]
-            tr = live.pop(("wt", m, h))
-            if h < 2:
-                eng_copy(WE_U.get(str(m), WE)[h], words_of(g)[:, h * 256:(h + 1) * 256, :], tr[:].rearrange("p w n -> p n w"))
-            else:
-                eng_copy(WE_U.get(str(m), WE)[2], words_of(g3), tr[:, :, 0:O2].rearrange("p w n -> p n w"))
 
-        def WQ(m):
-            g, g3 = live.pop(("wg", m))
-            nc.vector.quantize_mx(out=w2c[m][:].bitcast(FP8X4), scales=w2s[m][:], in_=g[:].rearrange("p n t -> p (n t)"))
-            nc.vector.quantize_mx(out=w3c[m][:].bitcast(FP8X4), scales=w3s[m][:], in_=g3[:].rearrange("p n t -> p (n t)"))
+        def unit(stage, u, *more):
+            if 0 <= u < UNITS:
+                stage(u, *more)
 
-        def scale_load():
-            if XROAD == "A1":
-                nc.sync.dma_start(out=sc[:, 0, :], in_=h1_scale.rearrange("a b k -> (a b k)").partition_broadcast(P))
-                for i in range(1, 4):
-                    nc.gpsimd.tensor_copy(out=sc[:, i, :], in_=sc[:, 0, :])
-            else:
-                nc.sync.dma_start(out=sc[:], in_=h1_scale.rearrange("a b (p t) -> p (a b t)", t=4))
+        def model(stage, m, *more):
+            if m < M:
+                stage(m, *more)
 
-        def b2_load():
-            nc.sync.dma_start(out=b2s[:], in_=b2.rearrange("m (p t) -> p m t", t=4))
+        def chunk(stage, u):
+            if u >= 0 and u % M == M - 1:
+                stage(u // M)
 
-        def b3_load():
-            nc.sync.dma_start(out=b3s[:].rearrange("p m o -> p (m o)"), in_=b3.rearrange("m o -> (m o)").partition_broadcast(P))
+        warm_up()
+        load_bytes(0)
+        load_scale()
+        load_weights(0)
+        load_bytes(1)
+        load_weights(1)
+        load_b2()
+        load_bytes(2)
+        load_b3()
+        widen(0)
+        widen(1)
+        turn_bytes(0, 0)
+        turn_weights(0, 0)
+        turn_weights(0, 1)
+        copy_weights(0, 0)
+        copy_weights(0, 1)
+        turn_bytes(0, 1)
+        turn_weights(0, 2)
+        copy_weights(0, 2)
+        multiply(0, 0)
+        multiply(0, 1)
+        quantize_h1(0)
+        quantize_weights(0)
 
-        def bias_sum():
-            nc.vector.tensor_reduce(out=bsum[:], in_=b3s[:].rearrange("p m o -> p o m"), axis=mybir.AxisListType.X, op=ALU.add)
-            nc.vector.tensor_scalar(out=bsum[:, 0:O], in0=bsum[:, 0:O], scalar1=1.0 / M, scalar2=None, op0=ALU.mult)
-            nc.vector.tensor_scalar(out=bsum[:, O:O2], in0=bsum[:, O:O2], scalar1=0.5 / M, scalar2=1e-6, op0=ALU.mult, op1=ALU.add)
+        for s in range(UNITS):
+            unit(first_matmul, s - 1)
+            model(load_weights, s + 2)
+            unit(hold_gpsimd, s - 3)
+            if s > 0:
+                multiply(s, 0)
+            chunk(finish_squares, s - 5)
+            unit(second_matmul, s - 3)
+            unit(relu, s - 1)
+            model(turn_weights, s + 1, 0)
+            unit(add_squares, s - 4)
+            model(copy_weights, s + 1, 0)
+            model(turn_weights, s + 1, 2)
+            model(turn_weights, s + 1, 1)
+            if s > 0:
+                multiply(s, 1)
+            model(copy_weights, s + 1, 1)
+            model(copy_weights, s + 1, 2)
+            unit(add_b3, s - 3)
+            chunk(sum_models, s - 4)
+            unit(interleave, s - 2)
+            if s > 0:
+                quantize_h1(s)
+            if s == 2:
+                average_b3()
+            unit(nonlinear, s - 3)
+            model(quantize_weights, s + 1)
+            unit(quantize_h2, s - 2)
+            unit(multiply_sigmoids, s - 4)
+            chunk(finish_partial, s - 5)
+            unit(turn_bytes, s + 1, 0)
+            chunk(finish_mean, s - 4)
+            unit(load_bytes, s + 3)
+            unit(widen, s + 2)
+            unit(turn_bytes, s + 1, 1)
 
-        def GG(u):
-            gt = pool.tile([P, 1], U32, name="gt", bufs=2)
-            nc.gpsimd.tensor_copy(out=gt[:], in_=live["h2", u][0][:, 0:1])
-
-        def run(op, u):
-            if op in ("WQ", "wload"):
-                if 0 <= u < M:
-                    {"WQ": WQ, "wload": wload}[op](u)
-            elif op[:2] in ("WT", "WE"):
-                if 0 <= u < M:
-                    {"WT": WT, "WE": WEV}[op[:2]](u, int(op[2]))
-            elif op in ("SUM", "FINA", "FINB", "FINC"):
-                if 0 <= u < NU and u % M == M - 1:
-                    {"SUM": SUM, "FINA": FINA, "FINB": FINB, "FINC": FINC}[op](u // M)
-            elif op in ("sc", "b2", "b3"):
-                {"sc": scale_load, "b2": b2_load, "b3": b3_load}[op]()
-            elif op == "LAST":
-                LAST(*u)
-            elif op == "LN":
-                LN(*u)
-            elif op == "LNTAB":
-                LNTAB()
-            elif op == "bsum":
-                if u == 0:
-                    bias_sum()
-            elif 0 <= u < NU:
-                f = {"load": load, "M1": M1, "M2": M2, "R": R, "Q1": Q1, "Q2": Q2, "E1": E1, "NL": NL, "PR": PR, "ACC": ACC, "GG": GG, "MR": MR}
-                if op in f:
-                    f[op](u)
-                else:
-                    g = {"P": Prod, "X": X, "EV": EV, "T": T, "C": cast, "I": I}[op[0] if op[:2] != "EV" else "EV"]
-                    a = op[2:] if op[:2] == "EV" else op[1:]
-                    g(u, int(a) if a in ("0", "1") else a)
-
-        for op, u in HEAD:
-            run(op, u)
-        for s in range(NU):
-            for op, d in ORDER:
-                run(op, s + d)
-        for op, u in TAIL:
-            run(op, u)
+        first_matmul(19)
+        interleave(18)
+        second_matmul(17)
+        add_b3(17)
+        quantize_h2(18)
+        second_matmul(18)
+        relu(19)
+        interleave(19)
+        nonlinear(17)
+        add_b3(18)
+        quantize_h2(19)
+        add_squares(16)
+        second_matmul(19)
+        multiply_sigmoids(16)
+        nonlinear(18)
+        add_squares(17)
+        add_b3(19)
+        sum_models(3)
+        nonlinear(19)
+        logarithm(0, 3)
+        multiply_sigmoids(17)
+        add_squares(18)
+        multiply_sigmoids(18)
+        multiply_sigmoids(19)
+        finish_mean(3)
+        add_squares(19)
+        finish_variance(0, 3)
+        logarithm(3, 4)
+        finish_squares(3)
+        finish_partial(3)
+        finish_variance(3, 4)

from contextlib import ExitStack

import concourse.mybir as mybir
from concourse.masks import make_identity

M, B, H, O = 5, 2048, 512, 64
O2 = 2 * O
P = 128
SLOTS = 4
CHUNK = SLOTS * P
CHUNKS = B // CHUNK
UNITS = CHUNKS * M
EPS = 1e-6
F32 = mybir.dt.float32
BF16 = mybir.dt.bfloat16
U8 = mybir.dt.uint8
U32 = mybir.dt.uint32
FP8 = mybir.dt.float8_e4m3fn
FP8X4 = mybir.dt.float8_e4m3fn_x4
AF = mybir.ActivationFunctionType
ALU = mybir.AluOpType
FLOPS = 2 * M * B * H * (H + O2)

WARM_UP_MATMULS = 4


def tile_gaussianmixturemlp_pa_kernel(tc, h1_bytes, h1_scale, W2, b2, W3, b3, out_0, out_1):
    nc = tc.nc
    with ExitStack() as ctx:
        const = ctx.enter_context(tc.tile_pool(name="const", bufs=1))
        pool = ctx.enter_context(tc.tile_pool(name="pool", bufs=3))
        psum = ctx.enter_context(tc.psum_pool(name="psum", bufs=1))
        ctx.enter_context(tc.manual_schedule())

        ident = const.tile([P, P], F32, name="ident")
        make_identity(nc, ident[:])
        scale = const.tile([P, 4], F32, name="scale")
        b2_cols = const.tile([P, M, 4], BF16, name="b2_cols")
        b3_rows = const.tile([P, M, O2], BF16, name="b3_rows")
        b3_mean = const.tile([P, O2], F32, name="b3_mean")
        w2_codes = [const.tile([P, H], U32, name=f"w2_codes{m}", align_bytes=64) for m in range(M)]
        w2_scales = [const.tile([P, H], U8, name=f"w2_scales{m}", align_bytes=64) for m in range(M)]
        w3_codes = [const.tile([P, O2], U32, name=f"w3_codes{m}", align_bytes=64) for m in range(M)]
        w3_scales = [const.tile([P, O2], U8, name=f"w3_scales{m}", align_bytes=64) for m in range(M)]
        sigmoids = const.tile([P, CHUNKS, SLOTS, O], F32, name="sigmoids")
        partial = const.tile([P, CHUNKS, SLOTS, O], F32, name="partial")
        logs = const.tile([P, CHUNKS, SLOTS, O], F32, name="logs")

        first = const.tile([P, 1], F32, name="first")
        nc.vector.memset(first[:], 0.0)
        nc.scalar.activation(out=first[:], in_=first[:], func=AF.Sigmoid)

        raw_bytes, wide, turned, products, h1_mx, banks, planes, mixed, h2_mx = {}, {}, {}, {}, {}, {}, {}, {}, {}
        y_banks, y_rows, squares, sigmoid_of, sums, ends, acc_of = {}, {}, {}, {}, {}, {}, {}
        w_raw, w_turned, w_mixed = {}, {}, {}


        def load_bytes(u):
            c, m = divmod(u, M)
            bytes_in = pool.tile([P, SLOTS * H], U8, name="bytes_in", bufs=4, align_bytes=64)
            src = h1_bytes[m, c * CHUNK:(c + 1) * CHUNK, :].rearrange("(p i) k -> p (i k)", i=SLOTS)
            pieces = 2 if u == 0 else 1
            width = SLOTS * H // pieces
            for a in range(0, SLOTS * H, width):
                nc.sync.dma_start(out=bytes_in[:, a:a + width], in_=src[:, a:a + width])
            raw_bytes[u] = bytes_in

        def load_weights(m):
            w2 = pool.tile([P, 4 * H], BF16, name="w2", align_bytes=64)
            src = W2[m].rearrange("(p t) k -> p (t k)", t=4)
            for a in range(0, 4 * H, 2 * H):
                nc.sync.dma_start(out=w2[:, a:a + 2 * H], in_=src[:, a:a + 2 * H])
            w3 = pool.tile([P, H], BF16, name="w3", align_bytes=64)
            nc.sync.dma_start(out=w3[:], in_=W3[m])
            w_raw[m] = (w2, w3)

        def load_scale():
            nc.sync.dma_start(out=scale[:], in_=h1_scale.rearrange("a b (p t) -> p (a b t)", t=4))

        def load_b2():
            nc.sync.dma_start(out=b2_cols[:], in_=b2.rearrange("m (p t) -> p m t", t=4))

        def load_b3():
            nc.sync.dma_start(out=b3_rows[:].rearrange("p m o -> p (m o)"),
                              in_=b3.rearrange("m o -> (m o)").partition_broadcast(P))

        def average_b3():
            nc.vector.tensor_reduce(out=b3_mean[:], in_=b3_rows[:].rearrange("p m o -> p o m"),
                                    axis=mybir.AxisListType.X, op=ALU.add)
            nc.vector.tensor_scalar(out=b3_mean[:, 0:O], in0=b3_mean[:, 0:O], scalar1=1.0 / M, scalar2=None, op0=ALU.mult)
            nc.vector.tensor_scalar(out=b3_mean[:, O:O2], in0=b3_mean[:, O:O2], scalar1=0.5 / M, scalar2=EPS,
                                    op0=ALU.mult, op1=ALU.add)


        def turn(rows, groups, first_group, tag, bufs):
            words = rows[:].bitcast(F32)
            bank = psum.tile([P, 2, 2 * P], F32, name=tag, bufs=bufs)
            for w in range(2):
                for g in range(groups):
                    start = (first_group + g) * (H // 2)
                    nc.tensor.transpose(bank[:, w, g * P:(g + 1) * P], words[:, start + w:start + H // 2:2], ident[:])
            return bank

        def word_pairs(tile):
            return tile[:].rearrange("p n t -> p (n t)").bitcast(F32).rearrange("p (n w) -> p n w", w=2)

        def turn_weights(m, part):
            w2, w3 = w_raw[m]
            if part < 2:
                w_turned[m, part] = turn(w2, 2, 2 * part, "mm", 4)
            else:
                w_turned[m, part] = turn(w3, 1, 0, "mm", 4)

        def copy_weights(m, part):
            if m not in w_mixed:
                w_mixed[m] = (pool.tile([P, H, 4], BF16, name="w2_mixed", align_bytes=64),
                              pool.tile([P, O2, 4], BF16, name="w3_mixed", align_bytes=64))
            w2_mixed, w3_mixed = w_mixed[m]
            bank = w_turned.pop((m, part))
            if part < 2:
                nc.scalar.copy(word_pairs(w2_mixed)[:, part * 2 * P:(part + 1) * 2 * P, :], bank[:].rearrange("p w n -> p n w"))
            else:
                nc.scalar.copy(word_pairs(w3_mixed), bank[:, :, 0:O2].rearrange("p w n -> p n w"))

        def quantize(codes, scales, mixed_tile):
            nc.vector.quantize_mx(out=codes[:].bitcast(FP8X4), scales=scales[:], in_=mixed_tile[:].rearrange("p n t -> p (n t)"))

        def quantize_weights(m):
            w2_mixed, w3_mixed = w_mixed.pop(m)
            quantize(w2_codes[m], w2_scales[m], w2_mixed)
            quantize(w3_codes[m], w3_scales[m], w3_mixed)


        def widen(u):
            wide[u] = pool.tile([P, SLOTS * H], BF16, name="wide", align_bytes=64)
            if u == 0:
                for i in range(SLOTS):
                    cols = slice(i * H, (i + 1) * H)
                    if i in (0, 3):
                        nc.scalar.copy(wide[u][:, cols], raw_bytes[u][:, cols].bitcast(FP8))
                    else:
                        nc.vector.tensor_copy(out=wide[u][:, cols], in_=raw_bytes[u][:, cols].bitcast(FP8))
            else:
                nc.scalar.copy(wide[u][:], raw_bytes[u][:].bitcast(FP8))

        def turn_bytes(u, half):
            turned[u, half] = turn(wide[u], 2, 2 * half, "turned", 2)

        def multiply(u, half):
            if half == 0:
                products[u] = pool.tile([P, CHUNK, 4], BF16, name="products", bufs=2, align_bytes=64)
            nc.vector.tensor_tensor(
                out=products[u][:, half * 2 * P:(half + 1) * 2 * P, :].rearrange("p n (w e) -> p n w e", e=2),
                in0=turned.pop((u, half))[:].bitcast(BF16).rearrange("p w (n e) -> p n w e", e=2),
                in1=scale[:].rearrange("p (w e) -> p w e", e=2).unsqueeze(1).to_broadcast([P, 2 * P, 2, 2]),
                op=ALU.mult)

        def quantize_h1(u):
            codes = pool.tile([P, CHUNK], U32, name="h1_codes", bufs=2, align_bytes=64)
            scales = pool.tile([P, CHUNK], U8, name="h1_scales", bufs=2, align_bytes=64)
            quantize(codes, scales, products.pop(u))
            h1_mx[u] = (codes, scales)

        def first_matmul(u):
            m = u % M
            codes, scales = h1_mx.pop(u)
            banks[u] = []
            for t in range(4):
                bank = psum.tile([P, CHUNK], F32, name="mm", bufs=4)
                cols = slice(t * P, (t + 1) * P)
                nc.tensor.matmul_mx(out=bank[:], lhsT=w2_codes[m][:, cols].bitcast(FP8X4), lhsT_scale=w2_scales[m][:, cols],
                                    rhs=codes[:].bitcast(FP8X4), rhs_scale=scales[:], start=True, stop=True)
                banks[u].append(bank)

        def relu(u):
            planes[u] = pool.tile([P, 4, CHUNK], BF16, name="planes", align_bytes=64)
            for t, bank in enumerate(banks.pop(u)):
                nc.scalar.activation(out=planes[u][:, t, :], in_=bank[:], func=AF.Relu, bias=b2_cols[:, u % M, t:t + 1])


        def hold_gpsimd(u):
            word = pool.tile([P, 1], U32, name="word", bufs=2)
            nc.gpsimd.tensor_copy(out=word[:], in_=h2_mx[u][0][:, 0:1])

        def interleave(u):
            mixed[u] = pool.tile([P, CHUNK, 4], BF16, name="mixed", bufs=2, align_bytes=64)
            if u < UNITS - 2:
                nc.gpsimd.tensor_scalar(out=mixed[u][:], in0=planes[u][:].rearrange("p t n -> p n t"),
                                        scalar1=1.0, scalar2=0.0, op0=ALU.mult, op1=ALU.add)
            else:
                share = CHUNK if u == UNITS - 2 else CHUNK // 2
                for a in range(0, CHUNK, share):
                    dst = mixed[u][:, a:a + share, :].rearrange("p (c i) t -> p c t i", i=4)
                    src = planes[u][:, :, a:a + share].rearrange("p t (c i) -> p c t i", i=4)
                    if a == 0:
                        nc.vector.tensor_copy(out=dst, in_=src)
                    else:
                        nc.scalar.copy(dst, src)

        def quantize_h2(u):
            codes = pool.tile([P, CHUNK], U32, name="h2_codes", bufs=2 * M, align_bytes=64)
            scales = pool.tile([P, CHUNK], U8, name="h2_scales", bufs=2 * M, align_bytes=64)
            quantize(codes, scales, mixed.pop(u))
            h2_mx[u] = (codes, scales)

        def second_pass(out, u, i, start, stop):
            m = u % M
            codes, scales = h2_mx[u]
            cols = slice(i * P, (i + 1) * P)
            nc.tensor.matmul_mx(out=out, lhsT=codes[:, cols].bitcast(FP8X4), lhsT_scale=scales[:, cols],
                                rhs=w3_codes[m][:].bitcast(FP8X4), rhs_scale=w3_scales[m][:], start=start, stop=stop)

        def second_matmul(u):
            y_banks[u] = psum.tile([P, SLOTS, O2], F32, name="y", bufs=1)
            for i in range(SLOTS):
                second_pass(y_banks[u][:, i, :], u, i, True, True)

        def sum_models(c):
            sums[c] = psum.tile([P, SLOTS, O2], F32, name="y", bufs=1)
            for i in range(SLOTS):
                for m in range(M):
                    second_pass(sums[c][:, i, :], c * M + m, i, m == 0, m == M - 1)


        def add_b3(u):
            y_rows[u] = pool.tile([P, SLOTS, O2], F32, name="y_rows")
            nc.vector.tensor_tensor(out=y_rows[u][:], in0=y_banks.pop(u)[:],
                                    in1=b3_rows[:, u % M, :].unsqueeze(1).to_broadcast([P, SLOTS, O2]), op=ALU.add)

        def nonlinear(u):
            c, m = divmod(u, M)
            y = y_rows.pop(u)
            squares[u] = pool.tile([P, 2, SLOTS, O], F32, name="squares")
            if m == 0:
                sigmoid_of[u] = sigmoids[:, c, :, :]
            else:
                sigmoid_tile = pool.tile([P, SLOTS, O], F32, name="sigmoid_tile")
                sigmoid_of[u] = sigmoid_tile[:]
            nc.scalar.activation(out=squares[u][:, 1, :, :], in_=y[:, :, O:O2], func=AF.Abs, scale=0.5)
            nc.scalar.activation(out=squares[u][:, 0, :, :], in_=y[:, :, 0:O], func=AF.Square)
            nc.scalar.activation(out=sigmoid_of[u], in_=squares[u][:, 1, :, :], func=AF.Sigmoid, scale=2.0)

        def multiply_sigmoids(u):
            c, m = divmod(u, M)
            factor = sigmoid_of.pop(u)
            if m > 0:
                nc.vector.tensor_tensor(out=sigmoids[:, c, :, :], in0=sigmoids[:, c, :, :], in1=factor, op=ALU.mult)

        def add_squares(u):
            c, m = divmod(u, M)
            if m == 0:
                acc_of[c] = psum.tile([P, 2 * SLOTS * O], F32, name="acc", bufs=1)
            nc.tensor.matmul(acc_of[c][:], ident[:], squares.pop(u)[:].rearrange("p j i o -> p (j i o)"),
                             start=(m == 0), stop=(m == M - 1))

        def finish_mean(c):
            averages = pool.tile([P, SLOTS, O2], F32, name="averages", bufs=2)
            total = sums.pop(c)
            for a, factor in ((0, 1.0 / M), (O, 0.5 / M)):
                nc.vector.scalar_tensor_tensor(out=averages[:, :, a:a + O], in0=total[:, :, a:a + O], scalar=factor,
                                               in1=b3_mean[:, a:a + O].unsqueeze(1).to_broadcast([P, SLOTS, O]),
                                               op0=ALU.mult, op1=ALU.add)
            nc.sync.dma_start(out=out_0[c * CHUNK:(c + 1) * CHUNK, :].rearrange("(p i) o -> p i o", i=SLOTS),
                              in_=averages[:, :, 0:O])
            mean_squared = pool.tile([P, SLOTS, O], F32, name="mean_squared", bufs=2)
            nc.scalar.activation(out=mean_squared[:], in_=averages[:, :, 0:O], func=AF.Square)
            ends[c] = (averages, mean_squared)

        def finish_squares(c):
            averages, mean_squared = ends[c]
            acc = acc_of.pop(c)[:].rearrange("p (j i o) -> p j i o", j=2, i=SLOTS)
            less = pool.tile([P, SLOTS, O], F32, name="less", bufs=2)
            nc.vector.scalar_tensor_tensor(out=less[:], in0=acc[:, 1, :, :], scalar=1.0 / M, in1=mean_squared[:],
                                           op0=ALU.mult, op1=ALU.subtract)
            more = pool.tile([P, SLOTS, O], F32, name="more", bufs=2)
            nc.vector.scalar_tensor_tensor(out=more[:], in0=acc[:, 0, :, :], scalar=1.0 / M, in1=less[:],
                                           op0=ALU.mult, op1=ALU.add)
            ends[c] = (averages, more)

        def finish_partial(c):
            averages, more = ends.pop(c)
            engine = nc.gpsimd if c < CHUNKS - 1 else nc.vector
            engine.tensor_tensor(out=partial[:, c, :, :], in0=averages[:, :, O:O2], in1=more[:], op=ALU.add)

        def logarithm(c0, c1):
            nc.scalar.activation(out=logs[:, c0:c1, :, :], in_=sigmoids[:, c0:c1, :, :], func=AF.Ln)

        def finish_variance(c0, c1):
            variance = pool.tile([P, CHUNKS - 1, SLOTS, O], F32, name="variance", bufs=2)
            clipped = pool.tile([P, CHUNKS - 1, SLOTS, O], F32, name="clipped", bufs=2)
            n = c1 - c0
            nc.vector.scalar_tensor_tensor(out=variance[:, 0:n, :, :], in0=logs[:, c0:c1, :, :], scalar=-1.0 / M,
                                           in1=partial[:, c0:c1, :, :], op0=ALU.mult, op1=ALU.add)
            nc.vector.tensor_scalar(out=clipped[:, 0:n, :, :], in0=variance[:, 0:n, :, :], scalar1=0.0, scalar2=EPS,
                                    op0=ALU.max, op1=ALU.add)
            for c in range(c0, c1):
                nc.sync.dma_start(out=out_1[c * CHUNK:(c + 1) * CHUNK, :].rearrange("(p i) o -> p i o", i=SLOTS),
                                  in_=clipped[:, c - c0, :, :])

        def warm_up():
            zeros = const.tile([P, CHUNK], BF16, name="zeros")
            nc.vector.memset(zeros[:], 0.0)
            bank = psum.tile([P, CHUNK], F32, name="y", bufs=1)
            for i in range(WARM_UP_MATMULS):
                nc.tensor.matmul(bank[:], zeros[:, 0:P], zeros[:], start=True, stop=True)


        def unit(stage, u, *more):
            if 0 <= u < UNITS:
                stage(u, *more)

        def model(stage, m, *more):
            if m < M:
                stage(m, *more)

        def chunk(stage, u):
            if u >= 0 and u % M == M - 1:
                stage(u // M)

        warm_up()
        load_bytes(0)
        load_scale()
        load_weights(0)
        load_bytes(1)
        load_weights(1)
        load_b2()
        load_bytes(2)
        load_b3()
        widen(0)
        widen(1)
        turn_bytes(0, 0)
        turn_weights(0, 0)
        turn_weights(0, 1)
        copy_weights(0, 0)
        copy_weights(0, 1)
        turn_bytes(0, 1)
        turn_weights(0, 2)
        copy_weights(0, 2)
        multiply(0, 0)
        multiply(0, 1)
        quantize_h1(0)
        quantize_weights(0)

        for s in range(UNITS):
            unit(first_matmul, s - 1)
            model(load_weights, s + 2)
            unit(hold_gpsimd, s - 3)
            if s > 0:
                multiply(s, 0)
            chunk(finish_squares, s - 5)
            unit(second_matmul, s - 3)
            unit(relu, s - 1)
            model(turn_weights, s + 1, 0)
            unit(add_squares, s - 4)
            model(copy_weights, s + 1, 0)
            model(turn_weights, s + 1, 2)
            model(turn_weights, s + 1, 1)
            if s > 0:
                multiply(s, 1)
            model(copy_weights, s + 1, 1)
            model(copy_weights, s + 1, 2)
            unit(add_b3, s - 3)
            chunk(sum_models, s - 4)
            unit(interleave, s - 2)
            if s > 0:
                quantize_h1(s)
            if s == 2:
                average_b3()
            unit(nonlinear, s - 3)
            model(quantize_weights, s + 1)
            unit(quantize_h2, s - 2)
            unit(multiply_sigmoids, s - 4)
            chunk(finish_partial, s - 5)
            unit(turn_bytes, s + 1, 0)
            chunk(finish_mean, s - 4)
            unit(load_bytes, s + 3)
            unit(widen, s + 2)
            unit(turn_bytes, s + 1, 1)

        first_matmul(19)
        interleave(18)
        second_matmul(17)
        add_b3(17)
        quantize_h2(18)
        second_matmul(18)
        relu(19)
        interleave(19)
        nonlinear(17)
        add_b3(18)
        quantize_h2(19)
        add_squares(16)
        second_matmul(19)
        multiply_sigmoids(16)
        nonlinear(18)
        add_squares(17)
        add_b3(19)
        sum_models(3)
        nonlinear(19)
        logarithm(0, 3)
        multiply_sigmoids(17)
        add_squares(18)
        multiply_sigmoids(18)
        multiply_sigmoids(19)
        finish_mean(3)
        add_squares(19)
        finish_variance(0, 3)
        logarithm(3, 4)
        finish_squares(3)
        finish_partial(3)
        finish_variance(3, 4)
